import numpy as np
import ml_dtypes


def mxq(x, axis, fmt="e4m3"):
    dtype, down = {"e4m3": (ml_dtypes.float8_e4m3fn, 7), "e5m2": (ml_dtypes.float8_e5m2, 14)}[fmt]
    v = np.moveaxis(np.asarray(x, np.float32).astype(ml_dtypes.bfloat16).astype(np.float64), axis, -1)
    blocks = v.reshape(v.shape[:-1] + (-1, 32))
    amax = np.abs(blocks).max(-1, keepdims=True)
    byte = np.maximum(np.where(amax > 0, np.frexp(amax)[1] - 1 + 127, 0) - down, 1)
    scale = np.exp2(byte - 127.0)
    codes = (blocks / scale).astype(np.float32).astype(dtype).astype(np.float64)
    return np.moveaxis((codes * scale).reshape(v.shape), -1, axis)


WIDE = False


def mx_kscale(k):
    if not WIDE:
        return np.ones(k)
    levels = np.array([10, -10, 5, -5, 0])
    if k % 512:
        return np.exp2(np.random.permutation(np.resize(levels, k // 32))).repeat(32)
    a = np.empty((k // 512, 16))
    for p in range(k // 512):
        a[p, :8] = np.random.permutation(np.resize(levels, 8))
        for g in range(8):
            far = levels[np.abs(levels - a[p, g]) >= 10]
            a[p, g + 8] = far[np.random.randint(len(far))]
    return np.exp2(a.ravel()).repeat(32)


BF16 = ml_dtypes.bfloat16


def bf(x):
    return np.asarray(x, np.float32).astype(BF16)


def f64(x):
    return np.asarray(x).astype(np.float64)


B, CL, CH, CK, CV, CO, H, W = 2, 1024, 2048, 256, 512, 1024, 24, 24
N = H * W
PSP = (1, 3, 6, 8)
EPS = 1e-5


def psp(x):
    b, c, h, w = x.shape
    return np.concatenate(
        [x.reshape(b, c, s, h // s, s, w // s).mean(axis=(3, 5)).reshape(b, c, s * s) for s in PSP], axis=2)


def draw0():
    s = mx_kscale(CL)
    return {"low_feats": bf(np.random.standard_normal((B, CL, H, W)) * s[None, :, None, None]),
            "wk": bf(np.random.standard_normal((CK, CL)) * 2.5 / np.sqrt(CL) / s[None, :]),
            "bk": bf(np.random.standard_normal(CK) * 0.3),
            "gk": bf(np.random.uniform(0.5, 1.5, CK)),
            "bek": bf(np.random.standard_normal(CK) * 0.3),
            "mk": bf(np.random.standard_normal(CK) * 0.3),
            "vk": bf(np.random.uniform(0.5, 1.5, CK)),
            "wv": bf(np.random.standard_normal((CV, CL)) * 3.0 / np.sqrt(CL) / s[None, :]),
            "bv": bf(np.random.standard_normal(CV) * 0.3)}


def core(low_feats, wk, bk, gk, bek, mk, vk, wv, bv):
    xq = mxq(f64(low_feats).reshape(B, CL, N), 1, "e4m3")
    v = (mxq(f64(wv), 1, "e4m3") @ xq) + f64(bv)[None, :, None]
    value = psp(v.reshape(B, CV, H, W)).transpose(0, 2, 1)
    u = (mxq(f64(wk), 1, "e4m3") @ xq) + f64(bk)[None, :, None]
    sc = f64(gk) / np.sqrt(f64(vk) + EPS)
    r = np.maximum((u - f64(mk)[None, :, None]) * sc[None, :, None] + f64(bek)[None, :, None], 0.0)
    key = psp(r.reshape(B, CK, H, W))
    return value, key


def e4m3fn_bytes(y):
    return np.clip(np.asarray(y, np.float64), -448.0, 448.0).astype(np.float32).astype(ml_dtypes.float8_e4m3fn).view(np.uint8)


def e4m3fn_values(b):
    return np.asarray(b, np.uint8).view(ml_dtypes.float8_e4m3fn).astype(np.float64)


def setup_inputs():
    d = draw0()
    x0 = np.asarray(d['low_feats']).astype(np.float64)
    s = (np.max(np.abs(x0), axis=(0, 2, 3), keepdims=True) / 448.0).astype(np.float32)
    out = {}
    for k, v in d.items():
        if k == 'low_feats':
            out['low_feats_bytes'] = e4m3fn_bytes(x0 / s.astype(np.float64))
            out['low_feats_scale'] = s
        else:
            out[k] = v
    return out


def reference(low_feats_bytes, low_feats_scale, wk, bk, gk, bek, mk, vk, wv, bv):
    return core(e4m3fn_values(low_feats_bytes) * low_feats_scale.astype(np.float64), wk, bk, gk, bek, mk, vk, wv, bv)

@@ -1,0 +1,295 @@
+from contextlib import ExitStack
+
+import concourse.mybir as mybir
+from concourse.masks import make_identity
+
+F32 = mybir.dt.float32
+BF16 = mybir.dt.bfloat16
+U8 = mybir.dt.uint8
+U32 = mybir.dt.uint32
+FP8 = mybir.dt.float8_e4m3fn
+FP8X4 = mybir.dt.float8_e4m3fn_x4
+ALU = mybir.AluOpType
+ACT = mybir.ActivationFunctionType
+AX = mybir.AxisListType
+
+P = 128
+NB = 2
+NPX = 576
+NLOC = 110
+EPS = 1e-5
+FLOPS = 2 * 1152 * 1024 * 768
+
+NCOL = 1280
+CLASSES = ((0, 0, 9, 3), (192, 4, 2, 2), (384, 3, 5, 1))
+LAYER0 = (0, 640, 1024)
+V_PLANES = ((0, 2), (0, 3), (1, 3))
+
+
+def tile_afnb_pa_kernel(tc, low_feats_bytes, low_feats_scale, wk, bk, gk, bek, mk, vk, wv, bv, out_0, out_1):
+    nc = tc.nc
+    with ExitStack() as ctx:
+        keep = ctx.enter_context(tc.tile_pool(name="keep", bufs=1))
+        psw = ctx.enter_context(tc.psum_pool(name="psw", bufs=2))
+        psa = ctx.enter_context(tc.psum_pool(name="psa", bufs=6))
+        ctx.enter_context(tc.manual_schedule())
+
+        sc = keep.tile([P, 8], F32, name="sc")
+        nc.sync.dma_start(
+            out=sc[:].rearrange("p (g t) -> p g t", g=2),
+            in_=low_feats_scale.rearrange("o (g p t) a c -> p (o g) (t a c)", g=2, p=P, t=4),
+        )
+        xsrc = low_feats_bytes.rearrange("b (g p t) h w -> g t p b (h w)", g=2, p=P, t=4)
+        xb = {}
+        for g, t in ((0, 0), (0, 2), (0, 1), (0, 3), (1, 0), (1, 1), (1, 2), (1, 3)):
+            xb[(g, t)] = keep.tile([P, NB, NPX], U8, name="xbytes%d%d" % (g, t))
+            nc.sync.dma_start(out=xb[(g, t)][:], in_=xsrc[g, t])
+        wsb = []
+        for m in range(6):
+            w_tile = keep.tile([P, 1024], BF16, name="wsb%d" % m)
+            src = wv[m * P:(m + 1) * P, :] if m < 4 else wk[(m - 4) * P:(m - 3) * P, :]
+            nc.sync.dma_start(out=w_tile[:], in_=src)
+            wsb.append(w_tile)
+        pb = keep.tile([P, 6, 16], BF16, name="pb")
+        with nc.allow_non_contiguous_dma(reason="per-channel vectors, one value to a partition"):
+            for j, vec in enumerate((bk, gk, bek, mk, vk)):
+                nc.sync.dma_start(out=pb[:, j, 0:2], in_=vec.rearrange("(c p) -> p c", p=P))
+            nc.sync.dma_start(out=pb[:, 5, 0:4], in_=bv.rearrange("(c p) -> p c", p=P))
+
+        ident = keep.tile([P, P], F32, name="ident")
+        make_identity(nc, ident[:])
+        warm = keep.tile([P, 1], F32, name="warm")
+        nc.vector.memset(warm[:], 1.0)
+        warm2 = keep.tile([P, 1], F32, name="warm2")
+        nc.scalar.activation(out=warm2[:], in_=warm[:], func=ACT.Relu)
+        xg = []
+        for g in range(2):
+            xg_tile = keep.tile([P, NCOL, 4], BF16, name="xg%d" % g, align_bytes=64)
+            nc.vector.memset(xg_tile[:, 576:640, :], 0.0)
+            nc.vector.memset(xg_tile[:, 1216:1280, :], 0.0)
+            xg.append(xg_tile)
+        ov = keep.tile([P, 4, NB, P], F32, name="ov")
+        nc.gpsimd.memset(ov[:, :, :, NLOC:P], 0.0)
+        mhalf = keep.tile([P, 2], F32, name="mhalf")
+        nc.gpsimd.memset(mhalf[:], -0.5)
+
+        wts = []
+        for m in range(6):
+            words = wsb[m][:].bitcast(F32)
+            wt = psa.tile([P, 2, 2, P], F32, tag="acc", name="wt%d" % m)
+            for g in range(2):
+                for u in range(2):
+                    nc.tensor.transpose(wt[:, g, u, :], words[:, 256 * g + u:256 * (g + 1):2], ident[:])
+            wts.append(wt)
+
+        xw = [keep.tile([P, 4, NB * NPX], BF16, name="xw%d" % g) for g in range(2)]
+        xc = [keep.tile([P, NCOL], U32, name="xc%d" % g, align_bytes=64) for g in range(2)]
+        xs = [keep.tile([P, NCOL], U8, name="xs%d" % g, align_bytes=64) for g in range(2)]
+
+        def widen(g, t):
+            src_ap = xb[(g, t)][:].rearrange("p b n -> p (b n)").bitcast(FP8)
+            col = sc[:, 4 * g + t:4 * g + t + 1]
+            if (g, t) in V_PLANES:
+                nc.vector.tensor_scalar(out=xw[g][:, t, :], in0=src_ap, scalar1=col, scalar2=None, op0=ALU.mult)
+            else:
+                nc.scalar.activation(out=xw[g][:, t, :], in_=src_ap, func=ACT.Copy, scale=col)
+
+        def interleave(g):
+            rows = xw[g][:].rearrange("p t (q h w) -> p q h w t", q=4, h=12, w=24)
+            for c0, r0, rstep, depth in CLASSES:
+                for i in range(depth):
+                    a = LAYER0[i] + c0
+                    nc.vector.tensor_copy(
+                        out=xg[g][:, a:a + 192, :].rearrange("p (q s w) t -> p q s w t", q=4, s=2, w=24),
+                        in_=rows[:, :, r0 + i:r0 + i + rstep + 1:rstep, :, :],
+                    )
+
+        def quantize_x(g, a, b):
+            nc.vector.quantize_mx(
+                out=xc[g][:, a:b].bitcast(FP8X4),
+                scales=xs[g][:, a:b],
+                in_=xg[g][:, a:b, :].rearrange("p c t -> p (c t)"),
+            )
+
+        wg = keep.tile([P, 6, 2, P, 4], BF16, name="wg", align_bytes=64)
+        wc = keep.tile([P, 6 * 2 * P], U32, name="wc", align_bytes=64)
+        wsc = keep.tile([P, 6 * 2 * P], U8, name="wsc", align_bytes=64)
+
+        def copy_w(m):
+            nc.scalar.copy(
+                out=wg[:, m].rearrange("p g r t -> p (g r t)").bitcast(F32).rearrange("p (g r u) -> p g r u", g=2, u=2),
+                in_=wts[m][:].rearrange("p g u r -> p g r u"),
+            )
+
+        def quantize_w(m0, m1):
+            nc.vector.quantize_mx(
+                out=wc[:, m0 * 256:m1 * 256].bitcast(FP8X4),
+                scales=wsc[:, m0 * 256:m1 * 256],
+                in_=wg[:, m0:m1].rearrange("p m g r t -> p (m g r t)"),
+            )
+
+        widen(0, 0)
+        widen(0, 2)
+        widen(0, 1)
+        widen(0, 3)
+        interleave(0)
+        widen(1, 0)
+        widen(1, 1)
+        widen(1, 2)
+        widen(1, 3)
+        quantize_x(0, 0, 1024)
+        quantize_x(0, 1024, 1280)
+        for m in range(6):
+            copy_w(m)
+        interleave(1)
+        quantize_w(0, 4)
+        quantize_x(1, 0, 1024)
+        quantize_x(1, 1024, 1280)
+        quantize_w(4, 6)
+
+        var = keep.tile([P, 2], F32, name="var")
+        nc.gpsimd.tensor_scalar(out=var[:], in0=pb[:, 4, 0:2], scalar1=EPS, scalar2=None, op0=ALU.add)
+        rstd = keep.tile([P, 2], F32, name="rstd")
+        nc.gpsimd.tensor_tensor(out=rstd[:], in0=var[:], in1=mhalf[:], op=ALU.pow)
+        bn_scale = keep.tile([P, 2], F32, name="bn_scale")
+        nc.gpsimd.tensor_tensor(out=bn_scale[:], in0=pb[:, 1, 0:2], in1=rstd[:], op=ALU.mult)
+        bn_d = keep.tile([P, 2], F32, name="bn_d")
+        nc.gpsimd.tensor_tensor(out=bn_d[:], in0=pb[:, 0, 0:2], in1=pb[:, 3, 0:2], op=ALU.subtract)
+        bn_e = keep.tile([P, 2], F32, name="bn_e")
+        nc.gpsimd.tensor_tensor(out=bn_e[:], in0=bn_d[:], in1=bn_scale[:], op=ALU.mult)
+        bn_bias = keep.tile([P, 2], F32, name="bn_bias")
+        nc.gpsimd.tensor_tensor(out=bn_bias[:], in0=bn_e[:], in1=pb[:, 2, 0:2], op=ALU.add)
+        bd = keep.tile([P, 3, 4], F32, name="bd")
+        for c in range(3):
+            nc.gpsimd.tensor_scalar(out=bd[:, c, :], in0=pb[:, 5, 0:4], scalar1=float(3 - c), scalar2=None, op0=ALU.mult)
+
+        def group(out, m, offsets, n):
+            passes = [(g, off) for g in range(2) for off in offsets]
+            for idx, (g, off) in enumerate(passes):
+                w0 = (2 * m + g) * P
+                nc.tensor.matmul_mx(
+                    out=out,
+                    lhsT=wc[:, w0:w0 + P].bitcast(FP8X4),
+                    lhsT_scale=wsc[:, w0:w0 + P],
+                    rhs=xc[g][:, off:off + n].bitcast(FP8X4),
+                    rhs_scale=xs[g][:, off:off + n],
+                    start=(idx == 0),
+                    stop=(idx == len(passes) - 1),
+                )
+
+        ev = keep.tile([P, 3, 6, 192], F32, name="ev")
+        s8 = keep.tile([P, 6, NB, 64], F32, name="s8")
+        s6 = keep.tile([P, 6, NB, 36], F32, name="s6")
+        s3 = keep.tile([P, 6, NB, 9], F32, name="s3")
+        s1 = keep.tile([P, 6, NB, 1], F32, name="s1")
+        ok = keep.tile([P, 2, NB, NLOC], F32, name="ok")
+
+        def pool_big(m0, m1):
+            o8 = s8[:, m0:m1].rearrange("p m b (h r w) -> p (m b h) r w", h=2, r=4, w=8)
+            nc.vector.tensor_reduce(
+                out=o8[:, :, 0:4:3, :],
+                in_=ev[:, 0, m0:m1, :].rearrange("p m (q s w j) -> p (m q) s w j", q=4, s=2, w=8, j=3),
+                axis=AX.X, op=ALU.add,
+            )
+            nc.vector.tensor_reduce(
+                out=s8[:, m0:m1].rearrange("p m b (h x) -> p (m b h) x", h=2, x=32)[:, :, 8:24],
+                in_=ev[:, 1:3, m0:m1, :].rearrange("p c m (q e j) -> p (m q) e c j", q=4, e=16, j=3),
+                axis=AX.XY, op=ALU.add,
+            )
+            o6 = s6[:, m0:m1].rearrange("p m b (h r w) -> p (m b h) r w", h=2, r=3, w=6)
+            outer = ev[:, 0:3:2, m0:m1, :].rearrange("p c m (q s w j) -> p s (m q) w c j", q=4, s=2, w=6, j=4)
+            for s in range(2):
+                nc.vector.tensor_reduce(out=o6[:, :, 2 * s, :], in_=outer[:, s], axis=AX.XY, op=ALU.add)
+            nc.vector.tensor_reduce(
+                out=o6[:, :, 1, :],
+                in_=ev[:, 1, m0:m1, :].rearrange("p m (q s w j) -> p (m q) w s j", q=4, s=2, w=6, j=4),
+                axis=AX.XY, op=ALU.add,
+            )
+
+        def scale_big(m0, m1, dst):
+            nc.scalar.activation(out=dst[:, :, :, 46:110], in_=s8[:, m0:m1], func=ACT.Copy, scale=1.0 / 9.0)
+            nc.scalar.activation(out=dst[:, :, :, 10:46], in_=s6[:, m0:m1], func=ACT.Copy, scale=1.0 / 16.0)
+
+        def pool_small(m0, m1, dst):
+            nc.vector.tensor_reduce(
+                out=s3[:, m0:m1].rearrange("p m b (x y) -> p (m b x) y", x=3, y=3),
+                in_=s6[:, m0:m1].rearrange("p m b (x a y c) -> p (m b x) y a c", x=3, a=2, y=3, c=2),
+                axis=AX.XY, op=ALU.add,
+            )
+            nc.vector.tensor_reduce(
+                out=s1[:, m0:m1].rearrange("p m b o -> p (m b) o"),
+                in_=s3[:, m0:m1].rearrange("p m b n -> p (m b) n"),
+                axis=AX.X, op=ALU.add,
+            )
+            nc.vector.tensor_scalar(out=dst[:, :, :, 1:10], in0=s3[:, m0:m1], scalar1=1.0 / 64.0, scalar2=None, op0=ALU.mult)
+            nc.vector.tensor_scalar(out=dst[:, :, :, 0:1], in0=s1[:, m0:m1], scalar1=1.0 / 576.0, scalar2=None, op0=ALU.mult)
+
+        def value_tile(m):
+            acc_a = psa.tile([P, 512], F32, tag="acc", name="va%d" % m)
+            acc_b = psa.tile([P, 512], F32, tag="acc", name="vb%d" % m)
+            group(acc_a[:, 0:256], m, (0, 640, 1024), 256)
+            group(acc_a[:, 256:384], m, (256, 896), 128)
+            group(acc_b[:, 0:256], m, (384,), 256)
+            for c, src_ap in enumerate((acc_a[:, 0:192], acc_a[:, 192:384], acc_b[:, 0:192])):
+                nc.scalar.activation(out=ev[:, c, m, :], in_=src_ap, func=ACT.Identity, bias=bd[:, c, m:m + 1], scale=1.0)
+
+        relu_out = {}
+
+        def key_tile(i):
+            m = 4 + i
+            k1 = psa.tile([P, 512], F32, tag="acc", name="k1_%d" % i)
+            k2 = psa.tile([P, 512], F32, tag="acc", name="k2_%d" % i)
+            k3 = psa.tile([P, 512], F32, tag="acc", name="k3_%d" % i)
+            group(k1[:, 0:256], m, (0,), 256)
+            group(k1[:, 256:384], m, (256,), 128)
+            group(k2[:, 0:256], m, (640,), 256)
+            group(k2[:, 256:384], m, (896,), 128)
+            group(k3[:, 0:256], m, (384,), 256)
+            group(k3[:, 256:512], m, (1024,), 256)
+            ra = keep.tile([P, 2, 192], F32, name="ra%d" % i)
+            rb = keep.tile([P, 2, 192], F32, name="rb%d" % i)
+            rc = keep.tile([P, 192], F32, name="rc%d" % i)
+            scale = bn_scale[:, i:i + 1]
+            bias = bn_bias[:, i:i + 1]
+            nc.scalar.activation(out=ra[:].rearrange("p c n -> p (c n)"), in_=k1[:, 0:384], func=ACT.Relu, bias=bias, scale=scale)
+            nc.scalar.activation(out=rb[:].rearrange("p c n -> p (c n)"), in_=k2[:, 0:384], func=ACT.Relu, bias=bias, scale=scale)
+            nc.scalar.activation(out=rc[:], in_=k3[:, 256:448], func=ACT.Relu, bias=bias, scale=scale)
+            nc.scalar.activation(out=ev[:, 2, m, :], in_=k3[:, 0:192], func=ACT.Relu, bias=bias, scale=scale)
+            relu_out[i] = (ra, rb, rc)
+
+        def key_adds(i):
+            m = 4 + i
+            ra, rb, rc = relu_out[i]
+            nc.vector.tensor_tensor(out=ev[:, 0:2, m, :], in0=ra[:], in1=rb[:], op=ALU.add)
+            nc.vector.tensor_tensor(out=ev[:, 0, m, :], in0=ev[:, 0, m, :], in1=rc[:], op=ALU.add)
+
+        value_tile(0)
+        value_tile(1)
+        pool_big(0, 1)
+        value_tile(2)
+        pool_big(1, 2)
+        value_tile(3)
+        pool_big(2, 3)
+        key_tile(0)
+        pool_big(3, 4)
+        scale_big(0, 4, ov)
+        pool_small(0, 4, ov)
+        key_tile(1)
+        key_adds(0)
+        pool_big(4, 5)
+        for b in range(NB):
+            vt = psw.tile([P, 512], F32, tag="vt", name="vt%d" % b)
+            for m in range(4):
+                nc.tensor.transpose(vt[:, m * P:(m + 1) * P], ov[:, m, b, :], ident[:])
+            vo = keep.tile([P, 512], F32, name="vo%d" % b)
+            nc.scalar.copy(out=vo[:], in_=vt[:])
+            nc.sync.dma_start(out=out_0[b], in_=vo[0:NLOC, :])
+        key_adds(1)
+        pool_big(5, 6)
+        scale_big(4, 6, ok)
+        pool_small(4, 6, ok)
+        for i in range(2):
+            nc.sync.dma_start(
+                out=out_1[:, i * P:(i + 1) * P, :].rearrange("b p l -> p b l"),
+                in_=ok[:, i, :, :],
+            )

@@ -23,7 +23,9 @@ FLOPS = 2 * 1152 * 1024 * 768
 NCOL = 1280
 CLASSES = ((0, 0, 9, 3), (192, 4, 2, 2), (384, 3, 5, 1))
 LAYER0 = (0, 640, 1024)
-V_PLANES = ((0, 2), (0, 3), (1, 3))
+V_PLANES = ((0, 1), (0, 2), (0, 3))
+W_ORDER = (4, 5, 0, 1, 2, 3)
+S_SHARE = ((1, 1), (2, 0))
 
 
 def tile_afnb_pa_kernel(tc, low_feats_bytes, low_feats_scale, wk, bk, gk, bek, mk, vk, wv, bv, out_0, out_1):
@@ -41,15 +43,14 @@ def tile_afnb_pa_kernel(tc, low_feats_bytes, low_feats_scale, wk, bk, gk, bek, m
         )
         xsrc = low_feats_bytes.rearrange("b (g p t) h w -> g t p b (h w)", g=2, p=P, t=4)
         xb = {}
-        for g, t in ((0, 0), (0, 2), (0, 1), (0, 3), (1, 0), (1, 1), (1, 2), (1, 3)):
+        for g, t in ((0, 0), (0, 1), (0, 2), (0, 3), (1, 0), (1, 1), (1, 2), (1, 3)):
             xb[(g, t)] = keep.tile([P, NB, NPX], U8, name="xbytes%d%d" % (g, t))
             nc.sync.dma_start(out=xb[(g, t)][:], in_=xsrc[g, t])
-        wsb = []
-        for m in range(6):
-            w_tile = keep.tile([P, 1024], BF16, name="wsb%d" % m)
+        wsb = {}
+        for m in W_ORDER:
+            wsb[m] = keep.tile([P, 1024], BF16, name="wsb%d" % m)
             src = wv[m * P:(m + 1) * P, :] if m < 4 else wk[(m - 4) * P:(m - 3) * P, :]
-            nc.sync.dma_start(out=w_tile[:], in_=src)
-            wsb.append(w_tile)
+            nc.sync.dma_start(out=wsb[m][:], in_=src)
         pb = keep.tile([P, 6, 16], BF16, name="pb")
         with nc.allow_non_contiguous_dma(reason="per-channel vectors, one value to a partition"):
             for j, vec in enumerate((bk, gk, bek, mk, vk)):
@@ -73,14 +74,14 @@ def tile_afnb_pa_kernel(tc, low_feats_bytes, low_feats_scale, wk, bk, gk, bek, m
         mhalf = keep.tile([P, 2], F32, name="mhalf")
         nc.gpsimd.memset(mhalf[:], -0.5)
 
-        wts = []
-        for m in range(6):
+        wts = {}
+        for m in W_ORDER:
             words = wsb[m][:].bitcast(F32)
             wt = psa.tile([P, 2, 2, P], F32, tag="acc", name="wt%d" % m)
             for g in range(2):
                 for u in range(2):
                     nc.tensor.transpose(wt[:, g, u, :], words[:, 256 * g + u:256 * (g + 1):2], ident[:])
-            wts.append(wt)
+            wts[m] = wt
 
         xw = [keep.tile([P, 4, NB * NPX], BF16, name="xw%d" % g) for g in range(2)]
         xc = [keep.tile([P, NCOL], U32, name="xc%d" % g, align_bytes=64) for g in range(2)]
@@ -94,15 +95,17 @@ def tile_afnb_pa_kernel(tc, low_feats_bytes, low_feats_scale, wk, bk, gk, bek, m
             else:
                 nc.scalar.activation(out=xw[g][:, t, :], in_=src_ap, func=ACT.Copy, scale=col)
 
-        def interleave(g):
+        def interleave(g, scalar_share):
             rows = xw[g][:].rearrange("p t (q h w) -> p q h w t", q=4, h=12, w=24)
-            for c0, r0, rstep, depth in CLASSES:
+            for c, (c0, r0, rstep, depth) in enumerate(CLASSES):
                 for i in range(depth):
                     a = LAYER0[i] + c0
-                    nc.vector.tensor_copy(
-                        out=xg[g][:, a:a + 192, :].rearrange("p (q s w) t -> p q s w t", q=4, s=2, w=24),
-                        in_=rows[:, :, r0 + i:r0 + i + rstep + 1:rstep, :, :],
-                    )
+                    dst = xg[g][:, a:a + 192, :].rearrange("p (q s w) t -> p q s w t", q=4, s=2, w=24)
+                    if (c, i) in scalar_share:
+                        for s in range(2):
+                            nc.scalar.copy(out=dst[:, :, s], in_=rows[:, :, r0 + i + s * rstep, :, :])
+                    else:
+                        nc.vector.tensor_copy(out=dst, in_=rows[:, :, r0 + i:r0 + i + rstep + 1:rstep, :, :])
 
         def quantize_x(g, a, b):
             nc.vector.quantize_mx(
@@ -128,24 +131,20 @@ def tile_afnb_pa_kernel(tc, low_feats_bytes, low_feats_scale, wk, bk, gk, bek, m
                 in_=wg[:, m0:m1].rearrange("p m g r t -> p (m g r t)"),
             )
 
-        widen(0, 0)
-        widen(0, 2)
-        widen(0, 1)
-        widen(0, 3)
-        interleave(0)
-        widen(1, 0)
-        widen(1, 1)
-        widen(1, 2)
-        widen(1, 3)
+        for t in range(4):
+            widen(0, t)
+        interleave(0, ())
+        for t in range(4):
+            widen(1, t)
         quantize_x(0, 0, 1024)
         quantize_x(0, 1024, 1280)
-        for m in range(6):
+        interleave(1, S_SHARE)
+        for m in W_ORDER:
             copy_w(m)
-        interleave(1)
-        quantize_w(0, 4)
         quantize_x(1, 0, 1024)
         quantize_x(1, 1024, 1280)
         quantize_w(4, 6)
+        quantize_w(0, 4)
 
         var = keep.tile([P, 2], F32, name="var")
         nc.gpsimd.tensor_scalar(out=var[:], in0=pb[:, 4, 0:2], scalar1=EPS, scalar2=None, op0=ALU.add)
@@ -233,7 +232,12 @@ def tile_afnb_pa_kernel(tc, low_feats_bytes, low_feats_scale, wk, bk, gk, bek, m
             for c, src_ap in enumerate((acc_a[:, 0:192], acc_a[:, 192:384], acc_b[:, 0:192])):
                 nc.scalar.activation(out=ev[:, c, m, :], in_=src_ap, func=ACT.Identity, bias=bd[:, c, m:m + 1], scale=1.0)
 
-        relu_out = {}
+        rk = keep.tile([P, 2, 2, 2, 192], F32, name="rk")
+        rk2 = keep.tile([P, 2, 192], F32, name="rk2")
+        ek = keep.tile([P, 3, 2, 192], F32, name="ek")
+        pk = keep.tile([P, 3, 2, 96], F32, name="pk")
+        g4 = keep.tile([P, 3, 2, 48], F32, name="g4")
+        g3 = keep.tile([P, 2, 2, 2, 32], F32, name="g3")
 
         def key_tile(i):
             m = 4 + i
@@ -246,23 +250,49 @@ def tile_afnb_pa_kernel(tc, low_feats_bytes, low_feats_scale, wk, bk, gk, bek, m
             group(k2[:, 256:384], m, (896,), 128)
             group(k3[:, 0:256], m, (384,), 256)
             group(k3[:, 256:512], m, (1024,), 256)
-            ra = keep.tile([P, 2, 192], F32, name="ra%d" % i)
-            rb = keep.tile([P, 2, 192], F32, name="rb%d" % i)
-            rc = keep.tile([P, 192], F32, name="rc%d" % i)
             scale = bn_scale[:, i:i + 1]
             bias = bn_bias[:, i:i + 1]
-            nc.scalar.activation(out=ra[:].rearrange("p c n -> p (c n)"), in_=k1[:, 0:384], func=ACT.Relu, bias=bias, scale=scale)
-            nc.scalar.activation(out=rb[:].rearrange("p c n -> p (c n)"), in_=k2[:, 0:384], func=ACT.Relu, bias=bias, scale=scale)
-            nc.scalar.activation(out=rc[:], in_=k3[:, 256:448], func=ACT.Relu, bias=bias, scale=scale)
-            nc.scalar.activation(out=ev[:, 2, m, :], in_=k3[:, 0:192], func=ACT.Relu, bias=bias, scale=scale)
-            relu_out[i] = (ra, rb, rc)
+            nc.scalar.activation(out=rk[:, 0, :, i, :], in_=k1[:, 0:384].rearrange("p (c n) -> p c n", c=2), func=ACT.Relu, bias=bias, scale=scale)
+            nc.scalar.activation(out=rk[:, 1, :, i, :], in_=k2[:, 0:384].rearrange("p (c n) -> p c n", c=2), func=ACT.Relu, bias=bias, scale=scale)
+            nc.scalar.activation(out=rk2[:, i, :], in_=k3[:, 256:448], func=ACT.Relu, bias=bias, scale=scale)
+            nc.scalar.activation(out=ek[:, 2, i, :], in_=k3[:, 0:192], func=ACT.Relu, bias=bias, scale=scale)
 
-        def key_adds(i):
-            m = 4 + i
-            ra, rb, rc = relu_out[i]
-            nc.vector.tensor_tensor(out=ev[:, 0:2, m, :], in0=ra[:], in1=rb[:], op=ALU.add)
-            nc.vector.tensor_tensor(out=ev[:, 0, m, :], in0=ev[:, 0, m, :], in1=rc[:], op=ALU.add)
+        def gadd(out, in0, in1):
+            nc.gpsimd.tensor_tensor(out=out, in0=in0, in1=in1, op=ALU.add)
 
+        def key_pool():
+            flat = "p c i n -> p (c i n)"
+            gadd(ek[:, 0:2].rearrange(flat), rk[:, 0].rearrange(flat), rk[:, 1].rearrange(flat))
+            gadd(ek[:, 0].rearrange("p i n -> p (i n)"), ek[:, 0].rearrange("p i n -> p (i n)"), rk2[:].rearrange("p i n -> p (i n)"))
+            e_all = ek[:].rearrange(flat)
+            p_all = pk[:].rearrange(flat)
+            gadd(p_all, e_all[:, 0:1152:2], e_all[:, 1:1152:2])
+            gadd(g4[:].rearrange(flat), p_all[:, 0:576:2], p_all[:, 1:576:2])
+            o8 = s8[:, 4:6].rearrange("p m b (h r x a) -> p a (m b h) r x", h=2, r=4, x=4, a=2)
+            e3 = ek[:, 0].rearrange("p i n -> p (i n)")
+            p3 = pk[:, 0].rearrange("p i n -> p (i n)")
+            shape3 = "p (z s x) -> p z s x"
+            gadd(o8[:, 0, :, 0:4:3, :], p3[:, 0:192:3].rearrange(shape3, s=2, x=4), e3[:, 2:384:6].rearrange(shape3, s=2, x=4))
+            gadd(o8[:, 1, :, 0:4:3, :], e3[:, 3:384:6].rearrange(shape3, s=2, x=4), p3[:, 2:192:3].rearrange(shape3, s=2, x=4))
+            e21 = ek[:, 1:3].rearrange(flat)
+            p21 = pk[:, 1:3].rearrange(flat)
+            gadd(g3[:, 0].rearrange(flat), p21[:, 0:384:3], e21[:, 2:768:6])
+            gadd(g3[:, 1].rearrange(flat), e21[:, 3:768:6], p21[:, 2:384:3])
+            for a in range(2):
+                gadd(
+                    o8[:, a, :, 1:3, :],
+                    g3[:, a, 0].rearrange("p i (q s x) -> p (i q) s x", q=4, s=2, x=4),
+                    g3[:, a, 1].rearrange("p i (q s x) -> p (i q) s x", q=4, s=2, x=4),
+                )
+            o6 = s6[:, 4:6].rearrange("p m b (h r w) -> p (m b h) r w", h=2, r=3, w=6)
+            shape6 = "p i (q s w) -> p (i q) s w"
+            gadd(o6[:, :, 0:3:2, :], g4[:, 0].rearrange(shape6, q=4, s=2, w=6), g4[:, 2].rearrange(shape6, q=4, s=2, w=6))
+            mid = g4[:, 1].rearrange(shape6, q=4, s=2, w=6)
+            gadd(o6[:, :, 1, :], mid[:, :, 0, :], mid[:, :, 1, :])
+
+        key_tile(0)
+        key_tile(1)
+        key_pool()
         value_tile(0)
         value_tile(1)
         pool_big(0, 1)
@@ -270,13 +300,9 @@ def tile_afnb_pa_kernel(tc, low_feats_bytes, low_feats_scale, wk, bk, gk, bek, m
         pool_big(1, 2)
         value_tile(3)
         pool_big(2, 3)
-        key_tile(0)
         pool_big(3, 4)
         scale_big(0, 4, ov)
         pool_small(0, 4, ov)
-        key_tile(1)
-        key_adds(0)
-        pool_big(4, 5)
         for b in range(NB):
             vt = psw.tile([P, 512], F32, tag="vt", name="vt%d" % b)
             for m in range(4):
@@ -284,8 +310,6 @@ def tile_afnb_pa_kernel(tc, low_feats_bytes, low_feats_scale, wk, bk, gk, bek, m
             vo = keep.tile([P, 512], F32, name="vo%d" % b)
             nc.scalar.copy(out=vo[:], in_=vt[:])
             nc.sync.dma_start(out=out_0[b], in_=vo[0:NLOC, :])
-        key_adds(1)
-        pool_big(5, 6)
         scale_big(4, 6, ok)
         pool_small(4, 6, ok)
         for i in range(2):

@@ -32,9 +32,11 @@ def tile_afnb_pa_kernel(tc, low_feats_bytes, low_feats_scale, wk, bk, gk, bek, m
     nc = tc.nc
     with ExitStack() as ctx:
         keep = ctx.enter_context(tc.tile_pool(name="keep", bufs=1))
-        psw = ctx.enter_context(tc.psum_pool(name="psw", bufs=2))
-        psa = ctx.enter_context(tc.psum_pool(name="psa", bufs=6))
+        psum = ctx.enter_context(tc.psum_pool(name="psum", bufs=8))
         ctx.enter_context(tc.manual_schedule())
+
+        def bank(name):
+            return psum.tile([P, 512], F32, tag="bank", name=name)
 
         sc = keep.tile([P, 8], F32, name="sc")
         nc.sync.dma_start(
@@ -43,19 +45,19 @@ def tile_afnb_pa_kernel(tc, low_feats_bytes, low_feats_scale, wk, bk, gk, bek, m
         )
         xsrc = low_feats_bytes.rearrange("b (g p t) h w -> g t p b (h w)", g=2, p=P, t=4)
         xb = {}
-        for g, t in ((0, 0), (0, 1), (0, 2), (0, 3), (1, 0), (1, 1), (1, 2), (1, 3)):
-            xb[(g, t)] = keep.tile([P, NB, NPX], U8, name="xbytes%d%d" % (g, t))
-            nc.sync.dma_start(out=xb[(g, t)][:], in_=xsrc[g, t])
+        for g in range(2):
+            for t in range(4):
+                xb[(g, t)] = keep.tile([P, NB, NPX], U8, name="xbytes%d%d" % (g, t))
+                nc.sync.dma_start(out=xb[(g, t)][:], in_=xsrc[g, t])
+        prow_bf = keep.tile([16, P], BF16, name="prow_bf")
+        for j, vec in enumerate((bk, gk, bek, mk, vk)):
+            nc.sync.dma_start(out=prow_bf[2 * j:2 * j + 2, :], in_=vec.rearrange("(c p) -> c p", p=P))
+        nc.sync.dma_start(out=prow_bf[10:14, :], in_=bv.rearrange("(c p) -> c p", p=P))
         wsb = {}
         for m in W_ORDER:
             wsb[m] = keep.tile([P, 1024], BF16, name="wsb%d" % m)
             src = wv[m * P:(m + 1) * P, :] if m < 4 else wk[(m - 4) * P:(m - 3) * P, :]
             nc.sync.dma_start(out=wsb[m][:], in_=src)
-        pb = keep.tile([P, 6, 16], BF16, name="pb")
-        with nc.allow_non_contiguous_dma(reason="per-channel vectors, one value to a partition"):
-            for j, vec in enumerate((bk, gk, bek, mk, vk)):
-                nc.sync.dma_start(out=pb[:, j, 0:2], in_=vec.rearrange("(c p) -> p c", p=P))
-            nc.sync.dma_start(out=pb[:, 5, 0:4], in_=bv.rearrange("(c p) -> p c", p=P))
 
         ident = keep.tile([P, P], F32, name="ident")
         make_identity(nc, ident[:])
@@ -65,23 +67,40 @@ def tile_afnb_pa_kernel(tc, low_feats_bytes, low_feats_scale, wk, bk, gk, bek, m
         nc.scalar.activation(out=warm2[:], in_=warm[:], func=ACT.Relu)
         xg = []
         for g in range(2):
-            xg_tile = keep.tile([P, NCOL, 4], BF16, name="xg%d" % g, align_bytes=64)
-            nc.vector.memset(xg_tile[:, 576:640, :], 0.0)
-            nc.vector.memset(xg_tile[:, 1216:1280, :], 0.0)
-            xg.append(xg_tile)
+            xg.append(keep.tile([P, NCOL, 4], BF16, name="xg%d" % g, align_bytes=64))
         ov = keep.tile([P, 4, NB, P], F32, name="ov")
         nc.gpsimd.memset(ov[:, :, :, NLOC:P], 0.0)
         mhalf = keep.tile([P, 2], F32, name="mhalf")
         nc.gpsimd.memset(mhalf[:], -0.5)
+        prow = keep.tile([P, P], F32, name="prow")
+        for a, b, pixels in ((0, 1, 576.0), (1, 10, 64.0), (10, 46, 16.0), (46, NLOC, 9.0), (NLOC, P, 1.0)):
+            nc.gpsimd.memset(prow[:, a:b], pixels)
+        nc.gpsimd.tensor_copy(out=prow[0:14, :], in_=prow_bf[0:14, :])
 
-        wts = {}
-        for m in W_ORDER:
-            words = wsb[m][:].bitcast(F32)
-            wt = psa.tile([P, 2, 2, P], F32, tag="acc", name="wt%d" % m)
-            for g in range(2):
-                for u in range(2):
-                    nc.tensor.transpose(wt[:, g, u, :], words[:, 256 * g + u:256 * (g + 1):2], ident[:])
-            wts[m] = wt
+        bn_scale = keep.tile([P, 2], F32, name="bn_scale")
+        bn_bias = keep.tile([P, 2], F32, name="bn_bias")
+        bd = keep.tile([P, 3, 4], F32, name="bd")
+        rn = keep.tile([P, 1], F32, name="rn")
+
+        def channel_constants():
+            prm_ps = bank("prm_ps")
+            nc.tensor.transpose(prm_ps[:, 0:P], prow[:], ident[:])
+            prm = keep.tile([P, 16], F32, name="prm")
+            nc.vector.tensor_copy(out=prm[:], in_=prm_ps[:, 0:16])
+            nc.vector.reciprocal(out=rn[:], in_=prm_ps[:, 16:17])
+
+            var = keep.tile([P, 2], F32, name="var")
+            nc.gpsimd.tensor_scalar(out=var[:], in0=prm[:, 8:10], scalar1=EPS, scalar2=None, op0=ALU.add)
+            rstd = keep.tile([P, 2], F32, name="rstd")
+            nc.gpsimd.tensor_tensor(out=rstd[:], in0=var[:], in1=mhalf[:], op=ALU.pow)
+            nc.gpsimd.tensor_tensor(out=bn_scale[:], in0=prm[:, 2:4], in1=rstd[:], op=ALU.mult)
+            bn_d = keep.tile([P, 2], F32, name="bn_d")
+            nc.gpsimd.tensor_tensor(out=bn_d[:], in0=prm[:, 0:2], in1=prm[:, 6:8], op=ALU.subtract)
+            bn_e = keep.tile([P, 2], F32, name="bn_e")
+            nc.gpsimd.tensor_tensor(out=bn_e[:], in0=bn_d[:], in1=bn_scale[:], op=ALU.mult)
+            nc.gpsimd.tensor_tensor(out=bn_bias[:], in0=bn_e[:], in1=prm[:, 4:6], op=ALU.add)
+            for c in range(3):
+                nc.gpsimd.tensor_scalar(out=bd[:, c, :], in0=prm[:, 10:14], scalar1=float(3 - c), scalar2=None, op0=ALU.mult)
 
         xw = [keep.tile([P, 4, NB * NPX], BF16, name="xw%d" % g) for g in range(2)]
         xc = [keep.tile([P, NCOL], U32, name="xc%d" % g, align_bytes=64) for g in range(2)]
@@ -117,11 +136,20 @@ def tile_afnb_pa_kernel(tc, low_feats_bytes, low_feats_scale, wk, bk, gk, bek, m
         wg = keep.tile([P, 6, 2, P, 4], BF16, name="wg", align_bytes=64)
         wc = keep.tile([P, 6 * 2 * P], U32, name="wc", align_bytes=64)
         wsc = keep.tile([P, 6 * 2 * P], U8, name="wsc", align_bytes=64)
+        wts = {}
+
+        def transpose_w(m):
+            words = wsb[m][:].bitcast(F32)
+            wts[m] = bank("wt%d" % m)
+            for g in range(2):
+                for u in range(2):
+                    j = 2 * g + u
+                    nc.tensor.transpose(wts[m][:, j * P:(j + 1) * P], words[:, 256 * g + u:256 * (g + 1):2], ident[:])
 
         def copy_w(m):
             nc.scalar.copy(
                 out=wg[:, m].rearrange("p g r t -> p (g r t)").bitcast(F32).rearrange("p (g r u) -> p g r u", g=2, u=2),
-                in_=wts[m][:].rearrange("p g u r -> p g r u"),
+                in_=wts[m][:].rearrange("p (g u r) -> p g r u", g=2, u=2),
             )
 
         def quantize_w(m0, m1):
@@ -131,189 +159,232 @@ def tile_afnb_pa_kernel(tc, low_feats_bytes, low_feats_scale, wk, bk, gk, bek, m
                 in_=wg[:, m0:m1].rearrange("p m g r t -> p (m g r t)"),
             )
 
-        for t in range(4):
-            widen(0, t)
-        interleave(0, ())
-        for t in range(4):
-            widen(1, t)
-        quantize_x(0, 0, 1024)
-        quantize_x(0, 1024, 1280)
-        interleave(1, S_SHARE)
-        for m in W_ORDER:
-            copy_w(m)
-        quantize_x(1, 0, 1024)
-        quantize_x(1, 1024, 1280)
-        quantize_w(4, 6)
-        quantize_w(0, 4)
-
-        var = keep.tile([P, 2], F32, name="var")
-        nc.gpsimd.tensor_scalar(out=var[:], in0=pb[:, 4, 0:2], scalar1=EPS, scalar2=None, op0=ALU.add)
-        rstd = keep.tile([P, 2], F32, name="rstd")
-        nc.gpsimd.tensor_tensor(out=rstd[:], in0=var[:], in1=mhalf[:], op=ALU.pow)
-        bn_scale = keep.tile([P, 2], F32, name="bn_scale")
-        nc.gpsimd.tensor_tensor(out=bn_scale[:], in0=pb[:, 1, 0:2], in1=rstd[:], op=ALU.mult)
-        bn_d = keep.tile([P, 2], F32, name="bn_d")
-        nc.gpsimd.tensor_tensor(out=bn_d[:], in0=pb[:, 0, 0:2], in1=pb[:, 3, 0:2], op=ALU.subtract)
-        bn_e = keep.tile([P, 2], F32, name="bn_e")
-        nc.gpsimd.tensor_tensor(out=bn_e[:], in0=bn_d[:], in1=bn_scale[:], op=ALU.mult)
-        bn_bias = keep.tile([P, 2], F32, name="bn_bias")
-        nc.gpsimd.tensor_tensor(out=bn_bias[:], in0=bn_e[:], in1=pb[:, 2, 0:2], op=ALU.add)
-        bd = keep.tile([P, 3, 4], F32, name="bd")
-        for c in range(3):
-            nc.gpsimd.tensor_scalar(out=bd[:, c, :], in0=pb[:, 5, 0:4], scalar1=float(3 - c), scalar2=None, op0=ALU.mult)
-
-        def group(out, m, offsets, n):
-            passes = [(g, off) for g in range(2) for off in offsets]
-            for idx, (g, off) in enumerate(passes):
-                w0 = (2 * m + g) * P
+        def passes(out, m, g, offsets, n, start, stop):
+            w0 = (2 * m + g) * P
+            for idx, off in enumerate(offsets):
                 nc.tensor.matmul_mx(
                     out=out,
                     lhsT=wc[:, w0:w0 + P].bitcast(FP8X4),
                     lhsT_scale=wsc[:, w0:w0 + P],
                     rhs=xc[g][:, off:off + n].bitcast(FP8X4),
                     rhs_scale=xs[g][:, off:off + n],
-                    start=(idx == 0),
-                    stop=(idx == len(passes) - 1),
+                    start=(start and idx == 0),
+                    stop=(stop and idx == len(offsets) - 1),
                 )
 
-        ev = keep.tile([P, 3, 6, 192], F32, name="ev")
+        def group(out, m, offsets, n):
+            passes(out, m, 0, offsets, n, True, False)
+            passes(out, m, 1, offsets, n, False, True)
+
+        ev = keep.tile([P, 3, 4, 192], F32, name="ev")
         s8 = keep.tile([P, 6, NB, 64], F32, name="s8")
         s6 = keep.tile([P, 6, NB, 36], F32, name="s6")
         s3 = keep.tile([P, 6, NB, 9], F32, name="s3")
         s1 = keep.tile([P, 6, NB, 1], F32, name="s1")
         ok = keep.tile([P, 2, NB, NLOC], F32, name="ok")
+        ek = [keep.tile([P, 3, 1, 192], F32, name="ek%d" % i) for i in range(2)]
+        rk1 = [keep.tile([P, 2, 1, 192], F32, name="rk1_%d" % i) for i in range(2)]
+        rk2 = [keep.tile([P, 1, 192], F32, name="rk2_%d" % i) for i in range(2)]
+        kbank = {}
 
-        def pool_big(m0, m1):
-            o8 = s8[:, m0:m1].rearrange("p m b (h r w) -> p (m b h) r w", h=2, r=4, w=8)
-            nc.vector.tensor_reduce(
-                out=o8[:, :, 0:4:3, :],
-                in_=ev[:, 0, m0:m1, :].rearrange("p m (q s w j) -> p (m q) s w j", q=4, s=2, w=8, j=3),
-                axis=AX.X, op=ALU.add,
-            )
-            nc.vector.tensor_reduce(
-                out=s8[:, m0:m1].rearrange("p m b (h x) -> p (m b h) x", h=2, x=32)[:, :, 8:24],
-                in_=ev[:, 1:3, m0:m1, :].rearrange("p c m (q e j) -> p (m q) e c j", q=4, e=16, j=3),
-                axis=AX.XY, op=ALU.add,
-            )
+        def pool_big(src, m0, m1, o8i, o8ii):
             o6 = s6[:, m0:m1].rearrange("p m b (h r w) -> p (m b h) r w", h=2, r=3, w=6)
-            outer = ev[:, 0:3:2, m0:m1, :].rearrange("p c m (q s w j) -> p s (m q) w c j", q=4, s=2, w=6, j=4)
-            for s in range(2):
-                nc.vector.tensor_reduce(out=o6[:, :, 2 * s, :], in_=outer[:, s], axis=AX.XY, op=ALU.add)
-            nc.vector.tensor_reduce(
-                out=o6[:, :, 1, :],
-                in_=ev[:, 1, m0:m1, :].rearrange("p m (q s w j) -> p (m q) w s j", q=4, s=2, w=6, j=4),
-                axis=AX.XY, op=ALU.add,
+            outer = src[:, 0:3:2].rearrange("p c m (q s w j) -> p s (m q) w c j", q=4, s=2, w=6, j=4)
+
+            def red(out, in_, axis):
+                return lambda: nc.vector.tensor_reduce(out=out, in_=in_, axis=axis, op=ALU.add)
+
+            return [
+                red(o8i, src[:, 0].rearrange("p m (q s w j) -> p (m q) s w j", q=4, s=2, w=8, j=3), AX.X),
+                red(o6[:, :, 1, :], src[:, 1].rearrange("p m (q s w j) -> p (m q) w s j", q=4, s=2, w=6, j=4), AX.XY),
+                red(o8ii, src[:, 1:3].rearrange("p c m (q e j) -> p (m q) e c j", q=4, e=16, j=3), AX.XY),
+                red(o6[:, :, 0, :], outer[:, 0], AX.XY),
+                red(o6[:, :, 2, :], outer[:, 1], AX.XY),
+            ]
+
+        def key_big(i):
+            m = 4 + i
+            return pool_big(
+                ek[i][:], m, m + 1,
+                s8[:, m:m + 1].rearrange("p m b (h r w) -> p (m b h) r w", h=2, r=4, w=8)[:, :, 0:4:3, :],
+                s8[:, m:m + 1].rearrange("p m b (h x) -> p (m b h) x", h=2, x=32)[:, :, 8:24],
             )
 
-        def scale_big(m0, m1, dst):
-            nc.scalar.activation(out=dst[:, :, :, 46:110], in_=s8[:, m0:m1], func=ACT.Copy, scale=1.0 / 9.0)
-            nc.scalar.activation(out=dst[:, :, :, 10:46], in_=s6[:, m0:m1], func=ACT.Copy, scale=1.0 / 16.0)
+        def value_big(m):
+            sec = ov[:, m:m + 1, :, 46:110]
+            return pool_big(
+                ev[:, :, m:m + 1, :], m, m + 1,
+                sec.rearrange("p m b (h r w) -> p (m b) h r w", h=2, r=4, w=8)[:, :, :, 0:4:3, :],
+                sec.rearrange("p m b (h x) -> p (m b) h x", h=2, x=32)[:, :, :, 8:24],
+            )
 
-        def pool_small(m0, m1, dst):
+        def sum3(m0, m1, out):
             nc.vector.tensor_reduce(
-                out=s3[:, m0:m1].rearrange("p m b (x y) -> p (m b x) y", x=3, y=3),
+                out=out,
                 in_=s6[:, m0:m1].rearrange("p m b (x a y c) -> p (m b x) y a c", x=3, a=2, y=3, c=2),
                 axis=AX.XY, op=ALU.add,
             )
-            nc.vector.tensor_reduce(
-                out=s1[:, m0:m1].rearrange("p m b o -> p (m b) o"),
-                in_=s3[:, m0:m1].rearrange("p m b n -> p (m b) n"),
-                axis=AX.X, op=ALU.add,
-            )
-            nc.vector.tensor_scalar(out=dst[:, :, :, 1:10], in0=s3[:, m0:m1], scalar1=1.0 / 64.0, scalar2=None, op0=ALU.mult)
-            nc.vector.tensor_scalar(out=dst[:, :, :, 0:1], in0=s1[:, m0:m1], scalar1=1.0 / 576.0, scalar2=None, op0=ALU.mult)
+
+        def sum1(m0, m1, out):
+            nc.vector.tensor_reduce(out=out, in_=s6[:, m0:m1].rearrange("p m b n -> p (m b) n"), axis=AX.X, op=ALU.add)
+
+        def key_small(i):
+            m = 4 + i
+            dst = ok[:, i:i + 1]
+            return [
+                lambda: sum3(m, m + 1, s3[:, m:m + 1].rearrange("p m b (x y) -> p (m b x) y", x=3, y=3)),
+                lambda: sum1(m, m + 1, s1[:, m:m + 1].rearrange("p m b o -> p (m b) o")),
+                lambda: nc.vector.tensor_scalar(out=dst[:, :, :, 1:10], in0=s3[:, m:m + 1], scalar1=1.0 / 64.0, scalar2=None, op0=ALU.mult),
+                lambda: nc.vector.tensor_scalar(out=dst[:, :, :, 0:1], in0=s1[:, m:m + 1], scalar1=1.0 / 576.0, scalar2=None, op0=ALU.mult),
+            ]
+
+        def key_scale_store(i, queue):
+            m = 4 + i
+            dst = ok[:, i:i + 1]
+            nc.scalar.activation(out=dst[:, :, :, 46:110], in_=s8[:, m:m + 1], func=ACT.Copy, scale=1.0 / 9.0)
+            nc.scalar.activation(out=dst[:, :, :, 10:46], in_=s6[:, m:m + 1], func=ACT.Copy, scale=1.0 / 16.0)
+            return lambda: queue.dma_start(out=out_1[:, i * P:(i + 1) * P, :].rearrange("b p l -> p b l"), in_=ok[:, i, :, :])
+
+        def value_small(m0, m1):
+            return [
+                lambda: sum3(m0, m1, ov[:, m0:m1, :, 1:10].rearrange("p m b n -> p (m b) n")),
+                lambda: sum1(m0, m1, ov[:, m0:m1, :, 0:1].rearrange("p m b n -> p (m b) n")),
+            ]
+
+        def weave(main, extra):
+            for idx in range(max(len(main), len(extra))):
+                if idx < len(main):
+                    main[idx]()
+                if idx < len(extra):
+                    extra[idx]()
 
         def value_tile(m):
-            acc_a = psa.tile([P, 512], F32, tag="acc", name="va%d" % m)
-            acc_b = psa.tile([P, 512], F32, tag="acc", name="vb%d" % m)
+            acc_a = bank("va%d" % m)
+            acc_b = bank("vb%d" % m)
             group(acc_a[:, 0:256], m, (0, 640, 1024), 256)
             group(acc_a[:, 256:384], m, (256, 896), 128)
             group(acc_b[:, 0:256], m, (384,), 256)
             for c, src_ap in enumerate((acc_a[:, 0:192], acc_a[:, 192:384], acc_b[:, 0:192])):
                 nc.scalar.activation(out=ev[:, c, m, :], in_=src_ap, func=ACT.Identity, bias=bd[:, c, m:m + 1], scale=1.0)
 
-        rk = keep.tile([P, 2, 2, 2, 192], F32, name="rk")
-        rk2 = keep.tile([P, 2, 192], F32, name="rk2")
-        ek = keep.tile([P, 3, 2, 192], F32, name="ek")
-        pk = keep.tile([P, 3, 2, 96], F32, name="pk")
-        g4 = keep.tile([P, 3, 2, 48], F32, name="g4")
-        g3 = keep.tile([P, 2, 2, 2, 32], F32, name="g3")
+        KEY_WINDOWS = ((0, 512), (512, 512), (1024, 256))
 
-        def key_tile(i):
-            m = 4 + i
-            k1 = psa.tile([P, 512], F32, tag="acc", name="k1_%d" % i)
-            k2 = psa.tile([P, 512], F32, tag="acc", name="k2_%d" % i)
-            k3 = psa.tile([P, 512], F32, tag="acc", name="k3_%d" % i)
-            group(k1[:, 0:256], m, (0,), 256)
-            group(k1[:, 256:384], m, (256,), 128)
-            group(k2[:, 0:256], m, (640,), 256)
-            group(k2[:, 256:384], m, (896,), 128)
-            group(k3[:, 0:256], m, (384,), 256)
-            group(k3[:, 256:512], m, (1024,), 256)
+        def key_passes(i, g):
+            if g == 0:
+                kbank[i] = [bank("k%d_%d" % (i, j)) for j in range(3)]
+            for j, (off, n) in enumerate(KEY_WINDOWS):
+                passes(kbank[i][j][:, 0:n], 4 + i, g, (off,), n, g == 0, g == 1)
+
+        def key_relu(i):
             scale = bn_scale[:, i:i + 1]
             bias = bn_bias[:, i:i + 1]
-            nc.scalar.activation(out=rk[:, 0, :, i, :], in_=k1[:, 0:384].rearrange("p (c n) -> p c n", c=2), func=ACT.Relu, bias=bias, scale=scale)
-            nc.scalar.activation(out=rk[:, 1, :, i, :], in_=k2[:, 0:384].rearrange("p (c n) -> p c n", c=2), func=ACT.Relu, bias=bias, scale=scale)
-            nc.scalar.activation(out=rk2[:, i, :], in_=k3[:, 256:448], func=ACT.Relu, bias=bias, scale=scale)
-            nc.scalar.activation(out=ek[:, 2, i, :], in_=k3[:, 0:192], func=ACT.Relu, bias=bias, scale=scale)
+            e_flat = ek[i][:].rearrange("p c i n -> p (c i n)")
+            k1, k2, k3 = kbank[i]
+            nc.scalar.activation(out=e_flat[:, 0:512], in_=k1[:, 0:512], func=ACT.Relu, bias=bias, scale=scale)
+            nc.scalar.activation(out=rk1[i][:].rearrange("p c i n -> p (c i n)"), in_=k2[:, 128:512], func=ACT.Relu, bias=bias, scale=scale)
+            nc.scalar.activation(out=rk2[i][:].rearrange("p i n -> p (i n)"), in_=k3[:, 0:192], func=ACT.Relu, bias=bias, scale=scale)
+            nc.scalar.activation(out=e_flat[:, 512:576], in_=k2[:, 0:64], func=ACT.Relu, bias=bias, scale=scale)
+
+        def key_adds(eng, i):
+            flat = "p i n -> p (i n)"
+            for c, other in ((0, rk1[i][:, 0]), (1, rk1[i][:, 1]), (0, rk2[i][:])):
+                eng.tensor_tensor(out=ek[i][:, c].rearrange(flat), in0=ek[i][:, c].rearrange(flat), in1=other.rearrange(flat), op=ALU.add)
+
+        pk = keep.tile([P, 3, 1, 96], F32, name="pk")
+        g4 = keep.tile([P, 3, 1, 48], F32, name="g4")
+        g3 = keep.tile([P, 2, 2, 1, 32], F32, name="g3")
 
         def gadd(out, in0, in1):
             nc.gpsimd.tensor_tensor(out=out, in0=in0, in1=in1, op=ALU.add)
 
-        def key_pool():
+        def key_pool_gpsimd(i):
+            m = 4 + i
             flat = "p c i n -> p (c i n)"
-            gadd(ek[:, 0:2].rearrange(flat), rk[:, 0].rearrange(flat), rk[:, 1].rearrange(flat))
-            gadd(ek[:, 0].rearrange("p i n -> p (i n)"), ek[:, 0].rearrange("p i n -> p (i n)"), rk2[:].rearrange("p i n -> p (i n)"))
-            e_all = ek[:].rearrange(flat)
+            e_all = ek[i][:].rearrange(flat)
             p_all = pk[:].rearrange(flat)
-            gadd(p_all, e_all[:, 0:1152:2], e_all[:, 1:1152:2])
-            gadd(g4[:].rearrange(flat), p_all[:, 0:576:2], p_all[:, 1:576:2])
-            o8 = s8[:, 4:6].rearrange("p m b (h r x a) -> p a (m b h) r x", h=2, r=4, x=4, a=2)
-            e3 = ek[:, 0].rearrange("p i n -> p (i n)")
-            p3 = pk[:, 0].rearrange("p i n -> p (i n)")
+            gadd(p_all, e_all[:, 0:576:2], e_all[:, 1:576:2])
+            gadd(g4[:].rearrange(flat), p_all[:, 0:288:2], p_all[:, 1:288:2])
+            o8 = s8[:, m:m + 1].rearrange("p m b (h r x a) -> p a (m b h) r x", h=2, r=4, x=4, a=2)
             shape3 = "p (z s x) -> p z s x"
-            gadd(o8[:, 0, :, 0:4:3, :], p3[:, 0:192:3].rearrange(shape3, s=2, x=4), e3[:, 2:384:6].rearrange(shape3, s=2, x=4))
-            gadd(o8[:, 1, :, 0:4:3, :], e3[:, 3:384:6].rearrange(shape3, s=2, x=4), p3[:, 2:192:3].rearrange(shape3, s=2, x=4))
-            e21 = ek[:, 1:3].rearrange(flat)
-            p21 = pk[:, 1:3].rearrange(flat)
-            gadd(g3[:, 0].rearrange(flat), p21[:, 0:384:3], e21[:, 2:768:6])
-            gadd(g3[:, 1].rearrange(flat), e21[:, 3:768:6], p21[:, 2:384:3])
+            gadd(o8[:, 0, :, 0:4:3, :], p_all[:, 0:96:3].rearrange(shape3, s=2, x=4), e_all[:, 2:192:6].rearrange(shape3, s=2, x=4))
+            gadd(o8[:, 1, :, 0:4:3, :], e_all[:, 3:192:6].rearrange(shape3, s=2, x=4), p_all[:, 2:96:3].rearrange(shape3, s=2, x=4))
+            gadd(g3[:, 0].rearrange(flat), p_all[:, 96:288:3], e_all[:, 194:576:6])
+            gadd(g3[:, 1].rearrange(flat), e_all[:, 195:576:6], p_all[:, 98:288:3])
+            shape8 = "p i (q s x) -> p (i q) s x"
             for a in range(2):
-                gadd(
-                    o8[:, a, :, 1:3, :],
-                    g3[:, a, 0].rearrange("p i (q s x) -> p (i q) s x", q=4, s=2, x=4),
-                    g3[:, a, 1].rearrange("p i (q s x) -> p (i q) s x", q=4, s=2, x=4),
-                )
-            o6 = s6[:, 4:6].rearrange("p m b (h r w) -> p (m b h) r w", h=2, r=3, w=6)
+                gadd(o8[:, a, :, 1:3, :], g3[:, a, 0].rearrange(shape8, q=4, s=2, x=4), g3[:, a, 1].rearrange(shape8, q=4, s=2, x=4))
+            o6 = s6[:, m:m + 1].rearrange("p m b (h r w) -> p (m b h) r w", h=2, r=3, w=6)
             shape6 = "p i (q s w) -> p (i q) s w"
             gadd(o6[:, :, 0:3:2, :], g4[:, 0].rearrange(shape6, q=4, s=2, w=6), g4[:, 2].rearrange(shape6, q=4, s=2, w=6))
             mid = g4[:, 1].rearrange(shape6, q=4, s=2, w=6)
             gadd(o6[:, :, 1, :], mid[:, :, 0, :], mid[:, :, 1, :])
 
-        key_tile(0)
-        key_tile(1)
-        key_pool()
+        vt = [None, None]
+        vo = keep.tile([P, NB, 512], F32, name="vo")
+
+        def value_turn(m0, m1):
+            nc.scalar.copy(out=ov[:, m0:m1, :, 10:46], in_=s6[:, m0:m1])
+            for b in range(NB):
+                if m0 == 0:
+                    vt[b] = bank("vt%d" % b)
+                for m in range(m0, m1):
+                    nc.tensor.transpose(vt[b][:, m * P:(m + 1) * P], ov[:, m, b, :], ident[:])
+
+        def value_out(m0, m1):
+            for b in range(NB):
+                nc.scalar.activation(out=vo[:, b, m0 * P:m1 * P], in_=vt[b][:, m0 * P:m1 * P], func=ACT.Copy, scale=rn[:, 0:1])
+            nc.sync.dma_start(out=out_0.rearrange("b l c -> l b c")[:, :, m0 * P:m1 * P], in_=vo[0:NLOC, :, m0 * P:m1 * P])
+
+        for t in range(4):
+            widen(0, t)
+        for g in range(2):
+            nc.vector.memset(xg[g][:, 576:640, :], 0.0)
+            nc.vector.memset(xg[g][:, 1216:1280, :], 0.0)
+        interleave(0, ())
+        channel_constants()
+        for t in range(4):
+            widen(1, t)
+        for m in W_ORDER:
+            transpose_w(m)
+        copy_w(4)
+        copy_w(5)
+        quantize_x(0, 1024, 1280)
+        quantize_x(0, 0, 1024)
+        interleave(1, S_SHARE)
+        quantize_w(4, 6)
+        key_passes(0, 0)
+        for m in range(4):
+            copy_w(m)
+        quantize_x(1, 1024, 1280)
+        quantize_x(1, 0, 1024)
+        key_passes(0, 1)
+        key_relu(0)
+        quantize_w(0, 4)
+        key_passes(1, 0)
+        key_passes(1, 1)
+        key_relu(1)
+        key_adds(nc.vector, 0)
+        big = key_big(0)
+        for idx in (1, 2, 0, 3, 4):
+            big[idx]()
+        key_adds(nc.gpsimd, 1)
+        key_pool_gpsimd(1)
         value_tile(0)
+        store_k0 = key_scale_store(0, nc.sync)
         value_tile(1)
-        pool_big(0, 1)
+        weave(value_big(0), key_small(0))
+        store_k0()
         value_tile(2)
-        pool_big(1, 2)
+        weave(value_big(1), [])
         value_tile(3)
-        pool_big(2, 3)
-        pool_big(3, 4)
-        scale_big(0, 4, ov)
-        pool_small(0, 4, ov)
-        for b in range(NB):
-            vt = psw.tile([P, 512], F32, tag="vt", name="vt%d" % b)
-            for m in range(4):
-                nc.tensor.transpose(vt[:, m * P:(m + 1) * P], ov[:, m, b, :], ident[:])
-            vo = keep.tile([P, 512], F32, name="vo%d" % b)
-            nc.scalar.copy(out=vo[:], in_=vt[:])
-            nc.sync.dma_start(out=out_0[b], in_=vo[0:NLOC, :])
-        scale_big(4, 6, ok)
-        pool_small(4, 6, ok)
-        for i in range(2):
-            nc.sync.dma_start(
-                out=out_1[:, i * P:(i + 1) * P, :].rearrange("b p l -> p b l"),
-                in_=ok[:, i, :, :],
-            )
+        weave(value_big(2), [])
+        big = value_big(3)
+        weave(big[0:2], value_small(0, 3))
+        value_turn(0, 3)
+        store_k1 = key_scale_store(1, nc.sync)
+        value_out(0, 3)
+        weave([big[3], big[4], big[2]], key_small(1)[0:2])
+        weave(value_small(3, 4), key_small(1)[2:4])
+        store_k1()
+        value_turn(3, 4)
+        value_out(3, 4)

@@ -70,6 +70,8 @@ def tile_afnb_pa_kernel(tc, low_feats_bytes, low_feats_scale, wk, bk, gk, bek, m
             xg.append(keep.tile([P, NCOL, 4], BF16, name="xg%d" % g, align_bytes=64))
         ov = keep.tile([P, 4, NB, P], F32, name="ov")
         nc.gpsimd.memset(ov[:, :, :, NLOC:P], 0.0)
+        okk = keep.tile([P, 2, NB, P], F32, name="okk")
+        nc.gpsimd.memset(okk[:, :, :, NLOC:P], 0.0)
         mhalf = keep.tile([P, 2], F32, name="mhalf")
         nc.gpsimd.memset(mhalf[:], -0.5)
         prow = keep.tile([P, P], F32, name="prow")
@@ -179,9 +181,8 @@ def tile_afnb_pa_kernel(tc, low_feats_bytes, low_feats_scale, wk, bk, gk, bek, m
         ev = keep.tile([P, 3, 4, 192], F32, name="ev")
         s8 = keep.tile([P, 6, NB, 64], F32, name="s8")
         s6 = keep.tile([P, 6, NB, 36], F32, name="s6")
-        s3 = keep.tile([P, 6, NB, 9], F32, name="s3")
-        s1 = keep.tile([P, 6, NB, 1], F32, name="s1")
-        ok = keep.tile([P, 2, NB, NLOC], F32, name="ok")
+        kts = keep.tile([P, 512], F32, name="kts")
+        kzs = keep.tile([P, 4, NLOC], F32, name="kzs")
         ek = [keep.tile([P, 3, 1, 192], F32, name="ek%d" % i) for i in range(2)]
         rk1 = [keep.tile([P, 2, 1, 192], F32, name="rk1_%d" % i) for i in range(2)]
         rk2 = [keep.tile([P, 1, 192], F32, name="rk2_%d" % i) for i in range(2)]
@@ -230,20 +231,41 @@ def tile_afnb_pa_kernel(tc, low_feats_bytes, low_feats_scale, wk, bk, gk, bek, m
 
         def key_small(i):
             m = 4 + i
-            dst = ok[:, i:i + 1]
             return [
-                lambda: sum3(m, m + 1, s3[:, m:m + 1].rearrange("p m b (x y) -> p (m b x) y", x=3, y=3)),
-                lambda: sum1(m, m + 1, s1[:, m:m + 1].rearrange("p m b o -> p (m b) o")),
-                lambda: nc.vector.tensor_scalar(out=dst[:, :, :, 1:10], in0=s3[:, m:m + 1], scalar1=1.0 / 64.0, scalar2=None, op0=ALU.mult),
-                lambda: nc.vector.tensor_scalar(out=dst[:, :, :, 0:1], in0=s1[:, m:m + 1], scalar1=1.0 / 576.0, scalar2=None, op0=ALU.mult),
+                lambda: sum3(m, m + 1, okk[:, i:i + 1, :, 1:10].rearrange("p m b n -> p (m b) n")),
+                lambda: sum1(m, m + 1, okk[:, i:i + 1, :, 0:1].rearrange("p m b n -> p (m b) n")),
             ]
 
-        def key_scale_store(i, queue):
+        def key_gather(i):
             m = 4 + i
-            dst = ok[:, i:i + 1]
-            nc.scalar.activation(out=dst[:, :, :, 46:110], in_=s8[:, m:m + 1], func=ACT.Copy, scale=1.0 / 9.0)
-            nc.scalar.activation(out=dst[:, :, :, 10:46], in_=s6[:, m:m + 1], func=ACT.Copy, scale=1.0 / 16.0)
-            return lambda: queue.dma_start(out=out_1[:, i * P:(i + 1) * P, :].rearrange("b p l -> p b l"), in_=ok[:, i, :, :])
+            nc.scalar.copy(out=okk[:, i:i + 1, :, 46:110], in_=s8[:, m:m + 1])
+            nc.scalar.copy(out=okk[:, i:i + 1, :, 10:46], in_=s6[:, m:m + 1])
+
+        kturn = {}
+
+        def key_turn1(i):
+            if i == 0:
+                kturn["kt"] = bank("kt")
+            for b in range(NB):
+                j = 2 * b + i
+                nc.tensor.transpose(kturn["kt"][:, j * P:(j + 1) * P], okk[:, i, b, :], ident[:])
+
+        def key_evac1(eng_is_vector, i):
+            src_ap = kturn["kt"][:].rearrange("p (b i cg cs) -> p cs b i cg", b=2, i=2, cs=4)[:, :, :, i, :]
+            dst_ap = kts[:].rearrange("p (cs b i cg) -> p cs b i cg", cs=4, b=2, i=2)[:, :, :, i, :]
+            if eng_is_vector:
+                nc.vector.tensor_scalar(out=dst_ap, in0=src_ap, scalar1=rn[:, 0:1], scalar2=None, op0=ALU.mult)
+            else:
+                nc.scalar.activation(out=dst_ap, in_=src_ap, func=ACT.Copy, scale=rn[:, 0:1])
+
+        def key_turn2():
+            kturn["kz"] = bank("kz")
+            for cs in range(4):
+                nc.tensor.transpose(kturn["kz"][:, cs * P:(cs + 1) * P], kts[:, cs * P:(cs + 1) * P], ident[:])
+
+        def key_out():
+            nc.vector.tensor_copy(out=kzs[:], in_=kturn["kz"][:].rearrange("p (cs l) -> p cs l", cs=4)[:, :, 0:NLOC])
+            nc.scalar.dma_start(out=out_1.rearrange("b (x cs) l -> (b x) (cs l)", cs=4), in_=kzs[:].rearrange("p cs l -> p (cs l)"))
 
         def value_small(m0, m1):
             return [
@@ -370,21 +392,25 @@ def tile_afnb_pa_kernel(tc, low_feats_bytes, low_feats_scale, wk, bk, gk, bek, m
         key_adds(nc.gpsimd, 1)
         key_pool_gpsimd(1)
         value_tile(0)
-        store_k0 = key_scale_store(0, nc.sync)
+        key_gather(0)
         value_tile(1)
         weave(value_big(0), key_small(0))
-        store_k0()
         value_tile(2)
         weave(value_big(1), [])
         value_tile(3)
+        key_turn1(0)
+        key_evac1(False, 0)
         weave(value_big(2), [])
         big = value_big(3)
         weave(big[0:2], value_small(0, 3))
         value_turn(0, 3)
-        store_k1 = key_scale_store(1, nc.sync)
+        key_gather(1)
         value_out(0, 3)
-        weave([big[3], big[4], big[2]], key_small(1)[0:2])
-        weave(value_small(3, 4), key_small(1)[2:4])
-        store_k1()
+        weave([big[3], big[4], big[2]], key_small(1))
+        weave(value_small(3, 4), [])
+        key_turn1(1)
+        key_evac1(True, 1)
         value_turn(3, 4)
+        key_turn2()
         value_out(3, 4)
+        key_out()

@@ -38,6 +38,9 @@ def tile_afnb_pa_kernel(tc, low_feats_bytes, low_feats_scale, wk, bk, gk, bek, m
         def bank(name):
             return psum.tile([P, 512], F32, tag="bank", name=name)
 
+        ident = keep.tile([P, P], F32, name="ident")
+        make_identity(nc, ident[:])
+
         sc = keep.tile([P, 8], F32, name="sc")
         nc.sync.dma_start(
             out=sc[:].rearrange("p (g t) -> p g t", g=2),
@@ -49,7 +52,9 @@ def tile_afnb_pa_kernel(tc, low_feats_bytes, low_feats_scale, wk, bk, gk, bek, m
             for t in range(4):
                 xb[(g, t)] = keep.tile([P, NB, NPX], U8, name="xbytes%d%d" % (g, t))
                 nc.sync.dma_start(out=xb[(g, t)][:], in_=xsrc[g, t])
-        prow_bf = keep.tile([16, P], BF16, name="prow_bf")
+        prow_bf = keep.tile([P, P], BF16, name="prow_bf")
+        for a, b, pixels in ((0, 1, 576.0), (1, 10, 64.0), (10, 46, 16.0), (46, NLOC, 9.0), (NLOC, P, 1.0)):
+            nc.gpsimd.memset(prow_bf[:, a:b], pixels)
         for j, vec in enumerate((bk, gk, bek, mk, vk)):
             nc.sync.dma_start(out=prow_bf[2 * j:2 * j + 2, :], in_=vec.rearrange("(c p) -> c p", p=P))
         nc.sync.dma_start(out=prow_bf[10:14, :], in_=bv.rearrange("(c p) -> c p", p=P))
@@ -59,12 +64,10 @@ def tile_afnb_pa_kernel(tc, low_feats_bytes, low_feats_scale, wk, bk, gk, bek, m
             src = wv[m * P:(m + 1) * P, :] if m < 4 else wk[(m - 4) * P:(m - 3) * P, :]
             nc.sync.dma_start(out=wsb[m][:], in_=src)
 
-        ident = keep.tile([P, P], F32, name="ident")
-        make_identity(nc, ident[:])
         warm = keep.tile([P, 1], F32, name="warm")
         nc.vector.memset(warm[:], 1.0)
         warm2 = keep.tile([P, 1], F32, name="warm2")
-        nc.scalar.activation(out=warm2[:], in_=warm[:], func=ACT.Relu)
+        nc.scalar.activation(out=warm2[:], in_=warm[:], func=ACT.Abs_reciprocal_sqrt)
         xg = []
         for g in range(2):
             xg.append(keep.tile([P, NCOL, 4], BF16, name="xg%d" % g, align_bytes=64))
@@ -72,37 +75,36 @@ def tile_afnb_pa_kernel(tc, low_feats_bytes, low_feats_scale, wk, bk, gk, bek, m
         nc.gpsimd.memset(ov[:, :, :, NLOC:P], 0.0)
         okk = keep.tile([P, 2, NB, P], F32, name="okk")
         nc.gpsimd.memset(okk[:, :, :, NLOC:P], 0.0)
-        mhalf = keep.tile([P, 2], F32, name="mhalf")
-        nc.gpsimd.memset(mhalf[:], -0.5)
-        prow = keep.tile([P, P], F32, name="prow")
-        for a, b, pixels in ((0, 1, 576.0), (1, 10, 64.0), (10, 46, 16.0), (46, NLOC, 9.0), (NLOC, P, 1.0)):
-            nc.gpsimd.memset(prow[:, a:b], pixels)
-        nc.gpsimd.tensor_copy(out=prow[0:14, :], in_=prow_bf[0:14, :])
+        epst = keep.tile([P, 1], F32, name="epst")
+        nc.gpsimd.memset(epst[:], EPS)
+        cmat = keep.tile([P, 32], BF16, name="cmat")
+        nc.gpsimd.tensor_copy(out=cmat[:, 0:17], in_=ident[:, 0:17])
+        nc.gpsimd.tensor_tensor(out=cmat[:, 17:19], in0=ident[:, 0:2], in1=ident[:, 6:8], op=ALU.subtract)
+        for c in range(3):
+            nc.gpsimd.tensor_scalar(out=cmat[:, 19 + 4 * c:23 + 4 * c], in0=ident[:, 10:14], scalar1=float(3 - c), scalar2=None, op0=ALU.mult)
+        for g in range(2):
+            nc.vector.memset(xg[g][:, 576:640, :], 0.0)
+            nc.vector.memset(xg[g][:, 1216:1280, :], 0.0)
 
         bn_scale = keep.tile([P, 2], F32, name="bn_scale")
         bn_bias = keep.tile([P, 2], F32, name="bn_bias")
-        bd = keep.tile([P, 3, 4], F32, name="bd")
+        prm = keep.tile([P, 32], F32, name="prm")
+        bd = prm[:, 19:31].rearrange("p (c m) -> p c m", c=3)
         rn = keep.tile([P, 1], F32, name="rn")
 
         def channel_constants():
             prm_ps = bank("prm_ps")
-            nc.tensor.transpose(prm_ps[:, 0:P], prow[:], ident[:])
-            prm = keep.tile([P, 16], F32, name="prm")
-            nc.vector.tensor_copy(out=prm[:], in_=prm_ps[:, 0:16])
-            nc.vector.reciprocal(out=rn[:], in_=prm_ps[:, 16:17])
+            nc.tensor.matmul(prm_ps[:, 0:31], lhsT=prow_bf[:], rhs=cmat[:, 0:31], start=True, stop=True)
+            return prm_ps
 
-            var = keep.tile([P, 2], F32, name="var")
-            nc.gpsimd.tensor_scalar(out=var[:], in0=prm[:, 8:10], scalar1=EPS, scalar2=None, op0=ALU.add)
+        def channel_constants_scalar(prm_ps):
+            nc.scalar.copy(out=prm[:, 0:31], in_=prm_ps[:, 0:31])
             rstd = keep.tile([P, 2], F32, name="rstd")
-            nc.gpsimd.tensor_tensor(out=rstd[:], in0=var[:], in1=mhalf[:], op=ALU.pow)
-            nc.gpsimd.tensor_tensor(out=bn_scale[:], in0=prm[:, 2:4], in1=rstd[:], op=ALU.mult)
-            bn_d = keep.tile([P, 2], F32, name="bn_d")
-            nc.gpsimd.tensor_tensor(out=bn_d[:], in0=prm[:, 0:2], in1=prm[:, 6:8], op=ALU.subtract)
-            bn_e = keep.tile([P, 2], F32, name="bn_e")
-            nc.gpsimd.tensor_tensor(out=bn_e[:], in0=bn_d[:], in1=bn_scale[:], op=ALU.mult)
-            nc.gpsimd.tensor_tensor(out=bn_bias[:], in0=bn_e[:], in1=prm[:, 4:6], op=ALU.add)
-            for c in range(3):
-                nc.gpsimd.tensor_scalar(out=bd[:, c, :], in0=prm[:, 10:14], scalar1=float(3 - c), scalar2=None, op0=ALU.mult)
+            nc.scalar.activation(out=rstd[:], in_=prm[:, 8:10], func=ACT.Abs_reciprocal_sqrt, bias=epst[:, 0:1], scale=1.0)
+            for i in range(2):
+                nc.scalar.activation(out=bn_scale[:, i:i + 1], in_=prm[:, 2 + i:3 + i], func=ACT.Copy, scale=rstd[:, i:i + 1])
+            for i in range(2):
+                nc.scalar.activation(out=bn_bias[:, i:i + 1], in_=prm[:, 17 + i:18 + i], func=ACT.Identity, bias=prm[:, 4 + i:5 + i], scale=bn_scale[:, i:i + 1])
 
         xw = [keep.tile([P, 4, NB * NPX], BF16, name="xw%d" % g) for g in range(2)]
         xc = [keep.tile([P, NCOL], U32, name="xc%d" % g, align_bytes=64) for g in range(2)]
@@ -359,13 +361,11 @@ def tile_afnb_pa_kernel(tc, low_feats_bytes, low_feats_scale, wk, bk, gk, bek, m
 
         for t in range(4):
             widen(0, t)
-        for g in range(2):
-            nc.vector.memset(xg[g][:, 576:640, :], 0.0)
-            nc.vector.memset(xg[g][:, 1216:1280, :], 0.0)
         interleave(0, ())
-        channel_constants()
+        prm_bank = channel_constants()
         for t in range(4):
             widen(1, t)
+        channel_constants_scalar(prm_bank)
         for m in W_ORDER:
             transpose_w(m)
         copy_w(4)
@@ -389,6 +389,7 @@ def tile_afnb_pa_kernel(tc, low_feats_bytes, low_feats_scale, wk, bk, gk, bek, m
         big = key_big(0)
         for idx in (1, 2, 0, 3, 4):
             big[idx]()
+        nc.vector.reciprocal(out=rn[:], in_=prm[:, 16:17])
         key_adds(nc.gpsimd, 1)
         key_pool_gpsimd(1)
         value_tile(0)

@@ -23,7 +23,7 @@ FLOPS = 2 * 1152 * 1024 * 768
 NCOL = 1280
 CLASSES = ((0, 0, 9, 3), (192, 4, 2, 2), (384, 3, 5, 1))
 LAYER0 = (0, 640, 1024)
-V_PLANES = ((0, 1), (0, 2), (0, 3))
+V_PLANES = ((0, 1), (0, 2), (0, 3), (1, 0))
 W_ORDER = (4, 5, 0, 1, 2, 3)
 S_SHARE = ((1, 1), (2, 0))
 

@@ -55,14 +55,6 @@ def tile_afnb_pa_kernel(tc, low_feats_bytes, low_feats_scale, wk, bk, gk, bek, m
         prow_bf = keep.tile([P, P], BF16, name="prow_bf")
         for a, b, pixels in ((0, 1, 576.0), (1, 10, 64.0), (10, 46, 16.0), (46, NLOC, 9.0), (NLOC, P, 1.0)):
             nc.gpsimd.memset(prow_bf[:, a:b], pixels)
-        for j, vec in enumerate((bk, gk, bek, mk, vk)):
-            nc.sync.dma_start(out=prow_bf[2 * j:2 * j + 2, :], in_=vec.rearrange("(c p) -> c p", p=P))
-        nc.sync.dma_start(out=prow_bf[10:14, :], in_=bv.rearrange("(c p) -> c p", p=P))
-        wsb = {}
-        for m in W_ORDER:
-            wsb[m] = keep.tile([P, 1024], BF16, name="wsb%d" % m)
-            src = wv[m * P:(m + 1) * P, :] if m < 4 else wk[(m - 4) * P:(m - 3) * P, :]
-            nc.sync.dma_start(out=wsb[m][:], in_=src)
 
         warm = keep.tile([P, 1], F32, name="warm")
         nc.vector.memset(warm[:], 1.0)
@@ -72,28 +64,39 @@ def tile_afnb_pa_kernel(tc, low_feats_bytes, low_feats_scale, wk, bk, gk, bek, m
         for g in range(2):
             xg.append(keep.tile([P, NCOL, 4], BF16, name="xg%d" % g, align_bytes=64))
         ov = keep.tile([P, 4, NB, P], F32, name="ov")
-        nc.gpsimd.memset(ov[:, :, :, NLOC:P], 0.0)
+        nc.vector.memset(ov[:, :, :, NLOC:P], 0.0)
         okk = keep.tile([P, 2, NB, P], F32, name="okk")
-        nc.gpsimd.memset(okk[:, :, :, NLOC:P], 0.0)
+        nc.vector.memset(okk[:, :, :, NLOC:P], 0.0)
         epst = keep.tile([P, 1], F32, name="epst")
-        nc.gpsimd.memset(epst[:], EPS)
+        nc.vector.memset(epst[:], EPS)
         cmat = keep.tile([P, 32], BF16, name="cmat")
-        nc.gpsimd.tensor_copy(out=cmat[:, 0:17], in_=ident[:, 0:17])
-        nc.gpsimd.tensor_tensor(out=cmat[:, 17:19], in0=ident[:, 0:2], in1=ident[:, 6:8], op=ALU.subtract)
-        for c in range(3):
-            nc.gpsimd.tensor_scalar(out=cmat[:, 19 + 4 * c:23 + 4 * c], in0=ident[:, 10:14], scalar1=float(3 - c), scalar2=None, op0=ALU.mult)
         for g in range(2):
             nc.vector.memset(xg[g][:, 576:640, :], 0.0)
             nc.vector.memset(xg[g][:, 1216:1280, :], 0.0)
+        nc.vector.tensor_copy(out=cmat[:, 0:17], in_=ident[:, 0:17])
+        nc.vector.tensor_tensor(out=cmat[:, 17:19], in0=ident[:, 0:2], in1=ident[:, 6:8], op=ALU.subtract)
+        for c in range(3):
+            nc.vector.tensor_scalar(out=cmat[:, 19 + 4 * c:23 + 4 * c], in0=ident[:, 10:14], scalar1=float(3 - c), scalar2=None, op0=ALU.mult)
 
         bn_scale = keep.tile([P, 2], F32, name="bn_scale")
         bn_bias = keep.tile([P, 2], F32, name="bn_bias")
         prm = keep.tile([P, 32], F32, name="prm")
         bd = prm[:, 19:31].rearrange("p (c m) -> p c m", c=3)
         rn = keep.tile([P, 1], F32, name="rn")
+        prm_ps = bank("prm_ps")
+        nc.tensor.matmul(prm_ps[:, 32:33], lhsT=prow_bf[:], rhs=cmat[:, 16:17], start=True, stop=True)
+        nc.vector.reciprocal(out=rn[:], in_=prm_ps[:, 32:33])
+
+        for j, vec in enumerate((bk, gk, bek, mk, vk)):
+            nc.sync.dma_start(out=prow_bf[2 * j:2 * j + 2, :], in_=vec.rearrange("(c p) -> c p", p=P))
+        nc.sync.dma_start(out=prow_bf[10:14, :], in_=bv.rearrange("(c p) -> c p", p=P))
+        wsb = {}
+        for m in W_ORDER:
+            wsb[m] = keep.tile([P, 1024], BF16, name="wsb%d" % m)
+            src = wv[m * P:(m + 1) * P, :] if m < 4 else wk[(m - 4) * P:(m - 3) * P, :]
+            nc.sync.dma_start(out=wsb[m][:], in_=src)
 
         def channel_constants():
-            prm_ps = bank("prm_ps")
             nc.tensor.matmul(prm_ps[:, 0:31], lhsT=prow_bf[:], rhs=cmat[:, 0:31], start=True, stop=True)
             return prm_ps
 
@@ -123,7 +126,7 @@ def tile_afnb_pa_kernel(tc, low_feats_bytes, low_feats_scale, wk, bk, gk, bek, m
             for c, (c0, r0, rstep, depth) in enumerate(CLASSES):
                 for i in range(depth):
                     a = LAYER0[i] + c0
-                    dst = xg[g][:, a:a + 192, :].rearrange("p (q s w) t -> p q s w t", q=4, s=2, w=24)
+                    dst = xg[g][:, a:a + 192, :].rearrange("p (s q w) t -> p q s w t", q=4, s=2, w=24)
                     if (c, i) in scalar_share:
                         for s in range(2):
                             nc.scalar.copy(out=dst[:, :, s], in_=rows[:, :, r0 + i + s * rstep, :, :])
@@ -190,36 +193,25 @@ def tile_afnb_pa_kernel(tc, low_feats_bytes, low_feats_scale, wk, bk, gk, bek, m
         rk2 = [keep.tile([P, 1, 192], F32, name="rk2_%d" % i) for i in range(2)]
         kbank = {}
 
-        def pool_big(src, m0, m1, o8i, o8ii):
-            o6 = s6[:, m0:m1].rearrange("p m b (h r w) -> p (m b h) r w", h=2, r=3, w=6)
-            outer = src[:, 0:3:2].rearrange("p c m (q s w j) -> p s (m q) w c j", q=4, s=2, w=6, j=4)
+        def pool_big(src, m, o8):
+            o6 = s6[:, m:m + 1].rearrange("p m b (h r w) -> p r (m b h) w", h=2, r=3, w=6)
 
             def red(out, in_, axis):
                 return lambda: nc.vector.tensor_reduce(out=out, in_=in_, axis=axis, op=ALU.add)
 
             return [
-                red(o8i, src[:, 0].rearrange("p m (q s w j) -> p (m q) s w j", q=4, s=2, w=8, j=3), AX.X),
-                red(o6[:, :, 1, :], src[:, 1].rearrange("p m (q s w j) -> p (m q) w s j", q=4, s=2, w=6, j=4), AX.XY),
-                red(o8ii, src[:, 1:3].rearrange("p c m (q e j) -> p (m q) e c j", q=4, e=16, j=3), AX.XY),
-                red(o6[:, :, 0, :], outer[:, 0], AX.XY),
-                red(o6[:, :, 2, :], outer[:, 1], AX.XY),
+                red(o8[:, 0:4:3], src[:, 0].rearrange("p m (e j) -> p (m e) j", j=3), AX.X),
+                red(o6[:, 1], src[:, 1].rearrange("p m (s q w j) -> p (m q) w s j", q=4, s=2, w=6, j=4), AX.XY),
+                red(o8[:, 1:3], src[:, 1:3].rearrange("p c m (e j) -> p (m e) c j", j=3), AX.XY),
+                red(o6[:, 0:3:2], src[:, 0:3:2].rearrange("p c m (e j) -> p (m e) c j", j=4), AX.XY),
             ]
 
         def key_big(i):
             m = 4 + i
-            return pool_big(
-                ek[i][:], m, m + 1,
-                s8[:, m:m + 1].rearrange("p m b (h r w) -> p (m b h) r w", h=2, r=4, w=8)[:, :, 0:4:3, :],
-                s8[:, m:m + 1].rearrange("p m b (h x) -> p (m b h) x", h=2, x=32)[:, :, 8:24],
-            )
+            return pool_big(ek[i][:], m, s8[:, m:m + 1].rearrange("p m b (h r w) -> p r (m b h) w", h=2, r=4, w=8))
 
         def value_big(m):
-            sec = ov[:, m:m + 1, :, 46:110]
-            return pool_big(
-                ev[:, :, m:m + 1, :], m, m + 1,
-                sec.rearrange("p m b (h r w) -> p (m b) h r w", h=2, r=4, w=8)[:, :, :, 0:4:3, :],
-                sec.rearrange("p m b (h x) -> p (m b) h x", h=2, x=32)[:, :, :, 8:24],
-            )
+            return pool_big(ev[:, :, m:m + 1, :], m, ov[:, m:m + 1, :, 46:110].rearrange("p m b (h r w) -> p r (m b) h w", h=2, r=4, w=8))
 
         def sum3(m0, m1, out):
             nc.vector.tensor_reduce(
@@ -235,13 +227,13 @@ def tile_afnb_pa_kernel(tc, low_feats_bytes, low_feats_scale, wk, bk, gk, bek, m
             m = 4 + i
             return [
                 lambda: sum3(m, m + 1, okk[:, i:i + 1, :, 1:10].rearrange("p m b n -> p (m b) n")),
-                lambda: sum1(m, m + 1, okk[:, i:i + 1, :, 0:1].rearrange("p m b n -> p (m b) n")),
             ]
 
         def key_gather(i):
             m = 4 + i
             nc.scalar.copy(out=okk[:, i:i + 1, :, 46:110], in_=s8[:, m:m + 1])
-            nc.scalar.copy(out=okk[:, i:i + 1, :, 10:46], in_=s6[:, m:m + 1])
+            for b in range(NB):
+                nc.scalar.activation(out=okk[:, i, b, 10:46], in_=s6[:, m, b, :], func=ACT.Copy, accum_out=okk[:, i, b, 0:1])
 
         kturn = {}
 
@@ -272,7 +264,6 @@ def tile_afnb_pa_kernel(tc, low_feats_bytes, low_feats_scale, wk, bk, gk, bek, m
         def value_small(m0, m1):
             return [
                 lambda: sum3(m0, m1, ov[:, m0:m1, :, 1:10].rearrange("p m b n -> p (m b) n")),
-                lambda: sum1(m0, m1, ov[:, m0:m1, :, 0:1].rearrange("p m b n -> p (m b) n")),
             ]
 
         def weave(main, extra):
@@ -329,16 +320,16 @@ def tile_afnb_pa_kernel(tc, low_feats_bytes, low_feats_scale, wk, bk, gk, bek, m
             gadd(p_all, e_all[:, 0:576:2], e_all[:, 1:576:2])
             gadd(g4[:].rearrange(flat), p_all[:, 0:288:2], p_all[:, 1:288:2])
             o8 = s8[:, m:m + 1].rearrange("p m b (h r x a) -> p a (m b h) r x", h=2, r=4, x=4, a=2)
-            shape3 = "p (z s x) -> p z s x"
+            shape3 = "p (s z x) -> p z s x"
             gadd(o8[:, 0, :, 0:4:3, :], p_all[:, 0:96:3].rearrange(shape3, s=2, x=4), e_all[:, 2:192:6].rearrange(shape3, s=2, x=4))
             gadd(o8[:, 1, :, 0:4:3, :], e_all[:, 3:192:6].rearrange(shape3, s=2, x=4), p_all[:, 2:96:3].rearrange(shape3, s=2, x=4))
             gadd(g3[:, 0].rearrange(flat), p_all[:, 96:288:3], e_all[:, 194:576:6])
             gadd(g3[:, 1].rearrange(flat), e_all[:, 195:576:6], p_all[:, 98:288:3])
-            shape8 = "p i (q s x) -> p (i q) s x"
+            shape8 = "p i (s q x) -> p (i q) s x"
             for a in range(2):
                 gadd(o8[:, a, :, 1:3, :], g3[:, a, 0].rearrange(shape8, q=4, s=2, x=4), g3[:, a, 1].rearrange(shape8, q=4, s=2, x=4))
             o6 = s6[:, m:m + 1].rearrange("p m b (h r w) -> p (m b h) r w", h=2, r=3, w=6)
-            shape6 = "p i (q s w) -> p (i q) s w"
+            shape6 = "p i (s q w) -> p (i q) s w"
             gadd(o6[:, :, 0:3:2, :], g4[:, 0].rearrange(shape6, q=4, s=2, w=6), g4[:, 2].rearrange(shape6, q=4, s=2, w=6))
             mid = g4[:, 1].rearrange(shape6, q=4, s=2, w=6)
             gadd(o6[:, :, 1, :], mid[:, :, 0, :], mid[:, :, 1, :])
@@ -347,7 +338,9 @@ def tile_afnb_pa_kernel(tc, low_feats_bytes, low_feats_scale, wk, bk, gk, bek, m
         vo = keep.tile([P, NB, 512], F32, name="vo")
 
         def value_turn(m0, m1):
-            nc.scalar.copy(out=ov[:, m0:m1, :, 10:46], in_=s6[:, m0:m1])
+            for m in range(m0, m1):
+                for b in range(NB):
+                    nc.scalar.activation(out=ov[:, m, b, 10:46], in_=s6[:, m, b, :], func=ACT.Copy, accum_out=ov[:, m, b, 0:1])
             for b in range(NB):
                 if m0 == 0:
                     vt[b] = bank("vt%d" % b)
@@ -361,9 +354,10 @@ def tile_afnb_pa_kernel(tc, low_feats_bytes, low_feats_scale, wk, bk, gk, bek, m
 
         for t in range(4):
             widen(0, t)
+        widen(1, 0)
         interleave(0, ())
         prm_bank = channel_constants()
-        for t in range(4):
+        for t in range(1, 4):
             widen(1, t)
         channel_constants_scalar(prm_bank)
         for m in W_ORDER:
@@ -387,9 +381,8 @@ def tile_afnb_pa_kernel(tc, low_feats_bytes, low_feats_scale, wk, bk, gk, bek, m
         key_relu(1)
         key_adds(nc.vector, 0)
         big = key_big(0)
-        for idx in (1, 2, 0, 3, 4):
+        for idx in (1, 2, 0, 3):
             big[idx]()
-        nc.vector.reciprocal(out=rn[:], in_=prm[:, 16:17])
         key_adds(nc.gpsimd, 1)
         key_pool_gpsimd(1)
         value_tile(0)
@@ -407,7 +400,7 @@ def tile_afnb_pa_kernel(tc, low_feats_bytes, low_feats_scale, wk, bk, gk, bek, m
         value_turn(0, 3)
         key_gather(1)
         value_out(0, 3)
-        weave([big[3], big[4], big[2]], key_small(1))
+        weave([big[3], big[2]], key_small(1))
         weave(value_small(3, 4), [])
         key_turn1(1)
         key_evac1(True, 1)

@@ -287,7 +287,8 @@ def tile_afnb_pa_kernel(tc, low_feats_bytes, low_feats_scale, wk, bk, gk, bek, m
         def key_passes(i, g):
             if g == 0:
                 kbank[i] = [bank("k%d_%d" % (i, j)) for j in range(3)]
-            for j, (off, n) in enumerate(KEY_WINDOWS):
+            for j in (2, 0, 1):
+                off, n = KEY_WINDOWS[j]
                 passes(kbank[i][j][:, 0:n], 4 + i, g, (off,), n, g == 0, g == 1)
 
         def key_relu(i):
@@ -295,44 +296,40 @@ def tile_afnb_pa_kernel(tc, low_feats_bytes, low_feats_scale, wk, bk, gk, bek, m
             bias = bn_bias[:, i:i + 1]
             e_flat = ek[i][:].rearrange("p c i n -> p (c i n)")
             k1, k2, k3 = kbank[i]
+            nc.scalar.activation(out=rk2[i][:].rearrange("p i n -> p (i n)"), in_=k3[:, 0:192], func=ACT.Relu, bias=bias, scale=scale)
             nc.scalar.activation(out=e_flat[:, 0:512], in_=k1[:, 0:512], func=ACT.Relu, bias=bias, scale=scale)
             nc.scalar.activation(out=rk1[i][:].rearrange("p c i n -> p (c i n)"), in_=k2[:, 128:512], func=ACT.Relu, bias=bias, scale=scale)
-            nc.scalar.activation(out=rk2[i][:].rearrange("p i n -> p (i n)"), in_=k3[:, 0:192], func=ACT.Relu, bias=bias, scale=scale)
             nc.scalar.activation(out=e_flat[:, 512:576], in_=k2[:, 0:64], func=ACT.Relu, bias=bias, scale=scale)
 
         def key_adds(eng, i):
             flat = "p i n -> p (i n)"
-            for c, other in ((0, rk1[i][:, 0]), (1, rk1[i][:, 1]), (0, rk2[i][:])):
+            for c, other in ((0, rk2[i][:]), (1, rk1[i][:, 1]), (0, rk1[i][:, 0])):
                 eng.tensor_tensor(out=ek[i][:, c].rearrange(flat), in0=ek[i][:, c].rearrange(flat), in1=other.rearrange(flat), op=ALU.add)
 
-        pk = keep.tile([P, 3, 1, 96], F32, name="pk")
-        g4 = keep.tile([P, 3, 1, 48], F32, name="g4")
-        g3 = keep.tile([P, 2, 2, 1, 32], F32, name="g3")
+        pk = keep.tile([P, 288], F32, name="pk")
+        g4 = keep.tile([P, 3, 48], F32, name="g4")
+        a3 = keep.tile([P, 192], F32, name="a3")
+        t12 = keep.tile([P, 2, 64], F32, name="t12")
 
         def gadd(out, in0, in1):
             nc.gpsimd.tensor_tensor(out=out, in0=in0, in1=in1, op=ALU.add)
 
         def key_pool_gpsimd(i):
             m = 4 + i
-            flat = "p c i n -> p (c i n)"
-            e_all = ek[i][:].rearrange(flat)
-            p_all = pk[:].rearrange(flat)
-            gadd(p_all, e_all[:, 0:576:2], e_all[:, 1:576:2])
-            gadd(g4[:].rearrange(flat), p_all[:, 0:288:2], p_all[:, 1:288:2])
-            o8 = s8[:, m:m + 1].rearrange("p m b (h r x a) -> p a (m b h) r x", h=2, r=4, x=4, a=2)
-            shape3 = "p (s z x) -> p z s x"
-            gadd(o8[:, 0, :, 0:4:3, :], p_all[:, 0:96:3].rearrange(shape3, s=2, x=4), e_all[:, 2:192:6].rearrange(shape3, s=2, x=4))
-            gadd(o8[:, 1, :, 0:4:3, :], e_all[:, 3:192:6].rearrange(shape3, s=2, x=4), p_all[:, 2:96:3].rearrange(shape3, s=2, x=4))
-            gadd(g3[:, 0].rearrange(flat), p_all[:, 96:288:3], e_all[:, 194:576:6])
-            gadd(g3[:, 1].rearrange(flat), e_all[:, 195:576:6], p_all[:, 98:288:3])
-            shape8 = "p i (s q x) -> p (i q) s x"
-            for a in range(2):
-                gadd(o8[:, a, :, 1:3, :], g3[:, a, 0].rearrange(shape8, q=4, s=2, x=4), g3[:, a, 1].rearrange(shape8, q=4, s=2, x=4))
+            e_all = ek[i][:].rearrange("p c i n -> p (c i n)")
+            gadd(pk[:], e_all[:, 0:576:2], e_all[:, 1:576:2])
+            gadd(g4[:].rearrange("p c n -> p (c n)"), pk[:, 0:288:2], pk[:, 1:288:2])
             o6 = s6[:, m:m + 1].rearrange("p m b (h r w) -> p (m b h) r w", h=2, r=3, w=6)
-            shape6 = "p i (s q w) -> p (i q) s w"
+            shape6 = "p (s q w) -> p q s w"
             gadd(o6[:, :, 0:3:2, :], g4[:, 0].rearrange(shape6, q=4, s=2, w=6), g4[:, 2].rearrange(shape6, q=4, s=2, w=6))
             mid = g4[:, 1].rearrange(shape6, q=4, s=2, w=6)
             gadd(o6[:, :, 1, :], mid[:, :, 0, :], mid[:, :, 1, :])
+            gadd(a3[:], e_all[:, 0:576:3], e_all[:, 1:576:3])
+            o8 = s8[:, m:m + 1].rearrange("p m b (h r w) -> p (m b h) r w", h=2, r=4, w=8)
+            shape8 = "p (s q w) -> p q s w"
+            gadd(o8[:, :, 0:4:3, :], a3[:, 0:64].rearrange(shape8, q=4, s=2, w=8), e_all[:, 2:192:3].rearrange(shape8, q=4, s=2, w=8))
+            gadd(t12[:].rearrange("p c n -> p (c n)"), a3[:, 64:192], e_all[:, 194:576:3])
+            gadd(o8[:, :, 1:3, :], t12[:, 0].rearrange(shape8, q=4, s=2, w=8), t12[:, 1].rearrange(shape8, q=4, s=2, w=8))
 
         vt = [None, None]
         vo = keep.tile([P, NB, 512], F32, name="vo")
@@ -372,7 +369,8 @@ def tile_afnb_pa_kernel(tc, low_feats_bytes, low_feats_scale, wk, bk, gk, bek, m
         for m in range(4):
             copy_w(m)
         quantize_x(1, 1024, 1280)
-        quantize_x(1, 0, 1024)
+        quantize_x(1, 0, 512)
+        quantize_x(1, 512, 1024)
         key_passes(0, 1)
         key_relu(0)
         quantize_w(0, 4)

@@ -65,8 +65,9 @@ def tile_afnb_pa_kernel(tc, low_feats_bytes, low_feats_scale, wk, bk, gk, bek, m
             xg.append(keep.tile([P, NCOL, 4], BF16, name="xg%d" % g, align_bytes=64))
         ov = keep.tile([P, 4, NB, P], F32, name="ov")
         nc.vector.memset(ov[:, :, :, NLOC:P], 0.0)
-        okk = keep.tile([P, 2, NB, P], F32, name="okk")
-        nc.vector.memset(okk[:, :, :, NLOC:P], 0.0)
+        okd = keep.tile([P, 2, NB, NLOC], F32, name="okd")
+        kacc = keep.tile([P, 2, NB, 1], F32, name="kacc")
+        k3 = keep.tile([P, 2, NB, 9], F32, name="k3")
         epst = keep.tile([P, 1], F32, name="epst")
         nc.vector.memset(epst[:], EPS)
         cmat = keep.tile([P, 32], BF16, name="cmat")
@@ -186,8 +187,6 @@ def tile_afnb_pa_kernel(tc, low_feats_bytes, low_feats_scale, wk, bk, gk, bek, m
         ev = keep.tile([P, 3, 4, 192], F32, name="ev")
         s8 = keep.tile([P, 6, NB, 64], F32, name="s8")
         s6 = keep.tile([P, 6, NB, 36], F32, name="s6")
-        kts = keep.tile([P, 512], F32, name="kts")
-        kzs = keep.tile([P, 4, NLOC], F32, name="kzs")
         ek = [keep.tile([P, 3, 1, 192], F32, name="ek%d" % i) for i in range(2)]
         rk1 = [keep.tile([P, 2, 1, 192], F32, name="rk1_%d" % i) for i in range(2)]
         rk2 = [keep.tile([P, 1, 192], F32, name="rk2_%d" % i) for i in range(2)]
@@ -226,40 +225,19 @@ def tile_afnb_pa_kernel(tc, low_feats_bytes, low_feats_scale, wk, bk, gk, bek, m
         def key_small(i):
             m = 4 + i
             return [
-                lambda: sum3(m, m + 1, okk[:, i:i + 1, :, 1:10].rearrange("p m b n -> p (m b) n")),
+                lambda: sum3(m, m + 1, k3[:, i:i + 1].rearrange("p m b n -> p (m b) n")),
             ]
 
-        def key_gather(i):
+        def key_means(i):
             m = 4 + i
-            nc.scalar.copy(out=okk[:, i:i + 1, :, 46:110], in_=s8[:, m:m + 1])
+            nc.scalar.activation(out=okd[:, i, :, 46:110], in_=s8[:, m], func=ACT.Copy, scale=1.0 / 9.0)
             for b in range(NB):
-                nc.scalar.activation(out=okk[:, i, b, 10:46], in_=s6[:, m, b, :], func=ACT.Copy, accum_out=okk[:, i, b, 0:1])
+                nc.scalar.activation(out=okd[:, i, b, 10:46], in_=s6[:, m, b, :], func=ACT.Copy, scale=1.0 / 16.0, accum_out=kacc[:, i, b, :])
+            nc.scalar.activation(out=okd[:, i, :, 0:1], in_=kacc[:, i], func=ACT.Copy, scale=1.0 / 36.0)
 
-        kturn = {}
-
-        def key_turn1(i):
-            if i == 0:
-                kturn["kt"] = bank("kt")
-            for b in range(NB):
-                j = 2 * b + i
-                nc.tensor.transpose(kturn["kt"][:, j * P:(j + 1) * P], okk[:, i, b, :], ident[:])
-
-        def key_evac1(eng_is_vector, i):
-            src_ap = kturn["kt"][:].rearrange("p (b i cg cs) -> p cs b i cg", b=2, i=2, cs=4)[:, :, :, i, :]
-            dst_ap = kts[:].rearrange("p (cs b i cg) -> p cs b i cg", cs=4, b=2, i=2)[:, :, :, i, :]
-            if eng_is_vector:
-                nc.vector.tensor_scalar(out=dst_ap, in0=src_ap, scalar1=rn[:, 0:1], scalar2=None, op0=ALU.mult)
-            else:
-                nc.scalar.activation(out=dst_ap, in_=src_ap, func=ACT.Copy, scale=rn[:, 0:1])
-
-        def key_turn2():
-            kturn["kz"] = bank("kz")
-            for cs in range(4):
-                nc.tensor.transpose(kturn["kz"][:, cs * P:(cs + 1) * P], kts[:, cs * P:(cs + 1) * P], ident[:])
-
-        def key_out():
-            nc.vector.tensor_copy(out=kzs[:], in_=kturn["kz"][:].rearrange("p (cs l) -> p cs l", cs=4)[:, :, 0:NLOC])
-            nc.scalar.dma_start(out=out_1.rearrange("b (x cs) l -> (b x) (cs l)", cs=4), in_=kzs[:].rearrange("p cs l -> p (cs l)"))
+        def key_store(i):
+            nc.scalar.activation(out=okd[:, i, :, 1:10], in_=k3[:, i], func=ACT.Copy, scale=1.0 / 64.0)
+            nc.scalar.dma_start(out=out_1.rearrange("b (i p) l -> i p b l", i=2)[i], in_=okd[:, i])
 
         def value_small(m0, m1):
             return [
@@ -332,22 +310,37 @@ def tile_afnb_pa_kernel(tc, low_feats_bytes, low_feats_scale, wk, bk, gk, bek, m
             gadd(o8[:, :, 1:3, :], t12[:, 0].rearrange(shape8, q=4, s=2, w=8), t12[:, 1].rearrange(shape8, q=4, s=2, w=8))
 
         vt = [None, None]
+        vlast = {}
         vo = keep.tile([P, NB, 512], F32, name="vo")
 
-        def value_turn(m0, m1):
+        def value_gather(m0, m1):
             for m in range(m0, m1):
                 for b in range(NB):
                     nc.scalar.activation(out=ov[:, m, b, 10:46], in_=s6[:, m, b, :], func=ACT.Copy, accum_out=ov[:, m, b, 0:1])
+
+        def value_turn():
             for b in range(NB):
-                if m0 == 0:
-                    vt[b] = bank("vt%d" % b)
-                for m in range(m0, m1):
+                vt[b] = bank("vt%d" % b)
+                for m in range(3):
                     nc.tensor.transpose(vt[b][:, m * P:(m + 1) * P], ov[:, m, b, :], ident[:])
 
-        def value_out(m0, m1):
+        def value_evac(b, on_vector):
+            if on_vector:
+                nc.vector.tensor_scalar(out=vo[:, b, 0:3 * P], in0=vt[b][:, 0:3 * P], scalar1=rn[:, 0:1], scalar2=None, op0=ALU.mult)
+            else:
+                nc.scalar.activation(out=vo[:, b, 0:3 * P], in_=vt[b][:, 0:3 * P], func=ACT.Copy, scale=rn[:, 0:1])
+
+        def value_store():
+            nc.sync.dma_start(out=out_0.rearrange("b l c -> l b c")[:, :, 0:3 * P], in_=vo[0:NLOC, :, 0:3 * P])
+
+        def value_turn_last():
+            vlast["t"] = bank("vt3")
             for b in range(NB):
-                nc.scalar.activation(out=vo[:, b, m0 * P:m1 * P], in_=vt[b][:, m0 * P:m1 * P], func=ACT.Copy, scale=rn[:, 0:1])
-            nc.sync.dma_start(out=out_0.rearrange("b l c -> l b c")[:, :, m0 * P:m1 * P], in_=vo[0:NLOC, :, m0 * P:m1 * P])
+                nc.tensor.transpose(vlast["t"][:, b * P:(b + 1) * P], ov[:, 3, b, :], ident[:])
+
+        def value_out_last():
+            nc.vector.tensor_scalar(out=vo[:, :, 3 * P:4 * P], in0=vlast["t"][:, 0:2 * P].rearrange("p (b c) -> p b c", b=NB), scalar1=rn[:, 0:1], scalar2=None, op0=ALU.mult)
+            nc.sync.dma_start(out=out_0.rearrange("b l c -> l b c")[:, :, 3 * P:4 * P], in_=vo[0:NLOC, :, 3 * P:4 * P])
 
         for t in range(4):
             widen(0, t)
@@ -384,25 +377,26 @@ def tile_afnb_pa_kernel(tc, low_feats_bytes, low_feats_scale, wk, bk, gk, bek, m
         key_adds(nc.gpsimd, 1)
         key_pool_gpsimd(1)
         value_tile(0)
-        key_gather(0)
         value_tile(1)
         weave(value_big(0), key_small(0))
         value_tile(2)
+        key_means(0)
+        key_store(0)
         weave(value_big(1), [])
         value_tile(3)
-        key_turn1(0)
-        key_evac1(False, 0)
         weave(value_big(2), [])
         big = value_big(3)
         weave(big[0:2], value_small(0, 3))
-        value_turn(0, 3)
-        key_gather(1)
-        value_out(0, 3)
-        weave([big[3], big[2]], key_small(1))
+        value_gather(0, 3)
+        value_turn()
+        weave([big[3], big[2]], [])
         weave(value_small(3, 4), [])
-        key_turn1(1)
-        key_evac1(True, 1)
-        value_turn(3, 4)
-        key_turn2()
-        value_out(3, 4)
-        key_out()
+        value_gather(3, 4)
+        value_turn_last()
+        weave(key_small(1), [])
+        value_evac(0, True)
+        value_evac(1, False)
+        value_store()
+        value_out_last()
+        key_means(1)
+        key_store(1)

@@ -25,7 +25,7 @@ CLASSES = ((0, 0, 9, 3), (192, 4, 2, 2), (384, 3, 5, 1))
 LAYER0 = (0, 640, 1024)
 V_PLANES = ((0, 1), (0, 2), (0, 3), (1, 0))
 W_ORDER = (4, 5, 0, 1, 2, 3)
-S_SHARE = ((1, 1), (2, 0))
+S_SHARE = ((2, 0), (1, 1))
 
 
 def tile_afnb_pa_kernel(tc, low_feats_bytes, low_feats_scale, wk, bk, gk, bek, mk, vk, wv, bv, out_0, out_1):
@@ -124,14 +124,17 @@ def tile_afnb_pa_kernel(tc, low_feats_bytes, low_feats_scale, wk, bk, gk, bek, m
 
         def interleave(g, scalar_share):
             rows = xw[g][:].rearrange("p t (q h w) -> p q h w t", q=4, h=12, w=24)
+            for c, i in scalar_share:
+                c0, r0, rstep, depth = CLASSES[c]
+                a = LAYER0[i] + c0
+                dst = xg[g][:, a:a + 192, :].rearrange("p (s q w) t -> p q s w t", q=4, s=2, w=24)
+                for s in range(2):
+                    nc.scalar.copy(out=dst[:, :, s], in_=rows[:, :, r0 + i + s * rstep, :, :])
             for c, (c0, r0, rstep, depth) in enumerate(CLASSES):
                 for i in range(depth):
                     a = LAYER0[i] + c0
                     dst = xg[g][:, a:a + 192, :].rearrange("p (s q w) t -> p q s w t", q=4, s=2, w=24)
-                    if (c, i) in scalar_share:
-                        for s in range(2):
-                            nc.scalar.copy(out=dst[:, :, s], in_=rows[:, :, r0 + i + s * rstep, :, :])
-                    else:
+                    if (c, i) not in scalar_share:
                         nc.vector.tensor_copy(out=dst, in_=rows[:, :, r0 + i:r0 + i + rstep + 1:rstep, :, :])
 
         def quantize_x(g, a, b):
@@ -265,7 +268,7 @@ def tile_afnb_pa_kernel(tc, low_feats_bytes, low_feats_scale, wk, bk, gk, bek, m
         def key_passes(i, g):
             if g == 0:
                 kbank[i] = [bank("k%d_%d" % (i, j)) for j in range(3)]
-            for j in (2, 0, 1):
+            for j in (0, 1, 2):
                 off, n = KEY_WINDOWS[j]
                 passes(kbank[i][j][:, 0:n], 4 + i, g, (off,), n, g == 0, g == 1)
 
@@ -274,14 +277,14 @@ def tile_afnb_pa_kernel(tc, low_feats_bytes, low_feats_scale, wk, bk, gk, bek, m
             bias = bn_bias[:, i:i + 1]
             e_flat = ek[i][:].rearrange("p c i n -> p (c i n)")
             k1, k2, k3 = kbank[i]
-            nc.scalar.activation(out=rk2[i][:].rearrange("p i n -> p (i n)"), in_=k3[:, 0:192], func=ACT.Relu, bias=bias, scale=scale)
             nc.scalar.activation(out=e_flat[:, 0:512], in_=k1[:, 0:512], func=ACT.Relu, bias=bias, scale=scale)
             nc.scalar.activation(out=rk1[i][:].rearrange("p c i n -> p (c i n)"), in_=k2[:, 128:512], func=ACT.Relu, bias=bias, scale=scale)
             nc.scalar.activation(out=e_flat[:, 512:576], in_=k2[:, 0:64], func=ACT.Relu, bias=bias, scale=scale)
+            nc.scalar.activation(out=rk2[i][:].rearrange("p i n -> p (i n)"), in_=k3[:, 0:192], func=ACT.Relu, bias=bias, scale=scale)
 
         def key_adds(eng, i):
             flat = "p i n -> p (i n)"
-            for c, other in ((0, rk2[i][:]), (1, rk1[i][:, 1]), (0, rk1[i][:, 0])):
+            for c, other in ((0, rk1[i][:, 0]), (1, rk1[i][:, 1]), (0, rk2[i][:])):
                 eng.tensor_tensor(out=ek[i][:, c].rearrange(flat), in0=ek[i][:, c].rearrange(flat), in1=other.rearrange(flat), op=ALU.add)
 
         pk = keep.tile([P, 288], F32, name="pk")
@@ -361,9 +364,9 @@ def tile_afnb_pa_kernel(tc, low_feats_bytes, low_feats_scale, wk, bk, gk, bek, m
         key_passes(0, 0)
         for m in range(4):
             copy_w(m)
-        quantize_x(1, 1024, 1280)
         quantize_x(1, 0, 512)
         quantize_x(1, 512, 1024)
+        quantize_x(1, 1024, 1280)
         key_passes(0, 1)
         key_relu(0)
         quantize_w(0, 4)

@@ -23,7 +23,7 @@ FLOPS = 2 * 1152 * 1024 * 768
 NCOL = 1280
 CLASSES = ((0, 0, 9, 3), (192, 4, 2, 2), (384, 3, 5, 1))
 LAYER0 = (0, 640, 1024)
-V_PLANES = ((0, 1), (0, 2), (0, 3), (1, 0))
+LOAD_ORDER = ((0, 0), (1, 0), (0, 1), (1, 1), (0, 2), (0, 3), (1, 2), (1, 3))
 W_ORDER = (4, 5, 0, 1, 2, 3)
 S_SHARE = ((2, 0), (1, 1))
 
@@ -48,10 +48,9 @@ def tile_afnb_pa_kernel(tc, low_feats_bytes, low_feats_scale, wk, bk, gk, bek, m
         )
         xsrc = low_feats_bytes.rearrange("b (g p t) h w -> g t p b (h w)", g=2, p=P, t=4)
         xb = {}
-        for g in range(2):
-            for t in range(4):
-                xb[(g, t)] = keep.tile([P, NB, NPX], U8, name="xbytes%d%d" % (g, t))
-                nc.sync.dma_start(out=xb[(g, t)][:], in_=xsrc[g, t])
+        for g, t in LOAD_ORDER:
+            xb[(g, t)] = keep.tile([P, NB, NPX], U8, name="xbytes%d%d" % (g, t))
+            nc.sync.dma_start(out=xb[(g, t)][:], in_=xsrc[g, t])
         prow_bf = keep.tile([P, P], BF16, name="prow_bf")
         for a, b, pixels in ((0, 1, 576.0), (1, 10, 64.0), (10, 46, 16.0), (46, NLOC, 9.0), (NLOC, P, 1.0)):
             nc.gpsimd.memset(prow_bf[:, a:b], pixels)
@@ -110,17 +109,26 @@ def tile_afnb_pa_kernel(tc, low_feats_bytes, low_feats_scale, wk, bk, gk, bek, m
             for i in range(2):
                 nc.scalar.activation(out=bn_bias[:, i:i + 1], in_=prm[:, 17 + i:18 + i], func=ACT.Identity, bias=prm[:, 4 + i:5 + i], scale=bn_scale[:, i:i + 1])
 
-        xw = [keep.tile([P, 4, NB * NPX], BF16, name="xw%d" % g) for g in range(2)]
+        xp = keep.tile([P, 2, NB * NPX, 2], BF16, name="xp")
+        xw = [None, keep.tile([P, 4, NB * NPX], BF16, name="xw1")]
         xc = [keep.tile([P, NCOL], U32, name="xc%d" % g, align_bytes=64) for g in range(2)]
         xs = [keep.tile([P, NCOL], U8, name="xs%d" % g, align_bytes=64) for g in range(2)]
 
         def widen(g, t):
             src_ap = xb[(g, t)][:].rearrange("p b n -> p (b n)").bitcast(FP8)
             col = sc[:, 4 * g + t:4 * g + t + 1]
-            if (g, t) in V_PLANES:
-                nc.vector.tensor_scalar(out=xw[g][:, t, :], in0=src_ap, scalar1=col, scalar2=None, op0=ALU.mult)
+            if g == 0:
+                nc.vector.tensor_scalar(out=xp[:, t // 2, :, t % 2], in0=src_ap, scalar1=col, scalar2=None, op0=ALU.mult)
             else:
                 nc.scalar.activation(out=xw[g][:, t, :], in_=src_ap, func=ACT.Copy, scale=col)
+
+        def interleave_words():
+            words = xp[:].rearrange("p u n e -> p (u n e)").bitcast(F32).rearrange("p (u q h w) -> p q h w u", u=2, q=4, h=12, w=24)
+            for c0, r0, rstep, depth in CLASSES:
+                for i in range(depth):
+                    a = LAYER0[i] + c0
+                    dst = xg[0][:, a:a + 192, :].rearrange("p c t -> p (c t)").bitcast(F32).rearrange("p (s q w u) -> p q s w u", q=4, s=2, w=24, u=2)
+                    nc.vector.tensor_copy(out=dst, in_=words[:, :, r0 + i:r0 + i + rstep + 1:rstep, :, :])
 
         def interleave(g, scalar_share):
             rows = xw[g][:].rearrange("p t (q h w) -> p q h w t", q=4, h=12, w=24)
@@ -347,10 +355,9 @@ def tile_afnb_pa_kernel(tc, low_feats_bytes, low_feats_scale, wk, bk, gk, bek, m
 
         for t in range(4):
             widen(0, t)
-        widen(1, 0)
-        interleave(0, ())
+        interleave_words()
         prm_bank = channel_constants()
-        for t in range(1, 4):
+        for t in range(4):
             widen(1, t)
         channel_constants_scalar(prm_bank)
         for m in W_ORDER:

@@ -376,7 +376,8 @@ def tile_afnb_pa_kernel(tc, low_feats_bytes, low_feats_scale, wk, bk, gk, bek, m
         quantize_x(1, 1024, 1280)
         key_passes(0, 1)
         key_relu(0)
-        quantize_w(0, 4)
+        quantize_w(0, 2)
+        quantize_w(2, 4)
         key_passes(1, 0)
         key_passes(1, 1)
         key_relu(1)

from contextlib import ExitStack

import concourse.mybir as mybir
from concourse.masks import make_identity

F32 = mybir.dt.float32
BF16 = mybir.dt.bfloat16
U8 = mybir.dt.uint8
U32 = mybir.dt.uint32
FP8 = mybir.dt.float8_e4m3fn
FP8X4 = mybir.dt.float8_e4m3fn_x4
ALU = mybir.AluOpType
ACT = mybir.ActivationFunctionType
AX = mybir.AxisListType

P = 128
NB = 2
NPX = 576
NLOC = 110
EPS = 1e-5
FLOPS = 2 * 1152 * 1024 * 768

NCOL = 1280
CLASSES = ((0, 0, 9, 3), (192, 4, 2, 2), (384, 3, 5, 1))
LAYER0 = (0, 640, 1024)
LOAD_ORDER = ((0, 0), (1, 0), (0, 1), (1, 1), (0, 2), (0, 3), (1, 2), (1, 3))
W_ORDER = (4, 5, 0, 1, 2, 3)
S_SHARE = ((2, 0), (1, 1))


def tile_afnb_pa_kernel(tc, low_feats_bytes, low_feats_scale, wk, bk, gk, bek, mk, vk, wv, bv, out_0, out_1):
    nc = tc.nc
    with ExitStack() as ctx:
        keep = ctx.enter_context(tc.tile_pool(name="keep", bufs=1))
        psum = ctx.enter_context(tc.psum_pool(name="psum", bufs=8))
        ctx.enter_context(tc.manual_schedule())

        def bank(name):
            return psum.tile([P, 512], F32, tag="bank", name=name)

        ident = keep.tile([P, P], F32, name="ident")
        make_identity(nc, ident[:])

        sc = keep.tile([P, 8], F32, name="sc")
        nc.sync.dma_start(
            out=sc[:].rearrange("p (g t) -> p g t", g=2),
            in_=low_feats_scale.rearrange("o (g p t) a c -> p (o g) (t a c)", g=2, p=P, t=4),
        )
        xsrc = low_feats_bytes.rearrange("b (g p t) h w -> g t p b (h w)", g=2, p=P, t=4)
        xb = {}
        for g, t in LOAD_ORDER:
            xb[(g, t)] = keep.tile([P, NB, NPX], U8, name="xbytes%d%d" % (g, t))
            nc.sync.dma_start(out=xb[(g, t)][:], in_=xsrc[g, t])
        prow_bf = keep.tile([P, P], BF16, name="prow_bf")
        for a, b, pixels in ((0, 1, 576.0), (1, 10, 64.0), (10, 46, 16.0), (46, NLOC, 9.0), (NLOC, P, 1.0)):
            nc.gpsimd.memset(prow_bf[:, a:b], pixels)

        warm = keep.tile([P, 1], F32, name="warm")
        nc.vector.memset(warm[:], 1.0)
        warm2 = keep.tile([P, 1], F32, name="warm2")
        nc.scalar.activation(out=warm2[:], in_=warm[:], func=ACT.Abs_reciprocal_sqrt)
        xg = []
        for g in range(2):
            xg.append(keep.tile([P, NCOL, 4], BF16, name="xg%d" % g, align_bytes=64))
        ov = keep.tile([P, 4, NB, P], F32, name="ov")
        nc.vector.memset(ov[:, :, :, NLOC:P], 0.0)
        okd = keep.tile([P, 2, NB, NLOC], F32, name="okd")
        kacc = keep.tile([P, 2, NB, 1], F32, name="kacc")
        k3 = keep.tile([P, 2, NB, 9], F32, name="k3")
        epst = keep.tile([P, 1], F32, name="epst")
        nc.vector.memset(epst[:], EPS)
        cmat = keep.tile([P, 32], BF16, name="cmat")
        for g in range(2):
            nc.vector.memset(xg[g][:, 576:640, :], 0.0)
            nc.vector.memset(xg[g][:, 1216:1280, :], 0.0)
        nc.vector.tensor_copy(out=cmat[:, 0:17], in_=ident[:, 0:17])
        nc.vector.tensor_tensor(out=cmat[:, 17:19], in0=ident[:, 0:2], in1=ident[:, 6:8], op=ALU.subtract)
        for c in range(3):
            nc.vector.tensor_scalar(out=cmat[:, 19 + 4 * c:23 + 4 * c], in0=ident[:, 10:14], scalar1=float(3 - c), scalar2=None, op0=ALU.mult)

        bn_scale = keep.tile([P, 2], F32, name="bn_scale")
        bn_bias = keep.tile([P, 2], F32, name="bn_bias")
        prm = keep.tile([P, 32], F32, name="prm")
        bd = prm[:, 19:31].rearrange("p (c m) -> p c m", c=3)
        rn = keep.tile([P, 1], F32, name="rn")
        prm_ps = bank("prm_ps")
        nc.tensor.matmul(prm_ps[:, 32:33], lhsT=prow_bf[:], rhs=cmat[:, 16:17], start=True, stop=True)
        nc.vector.reciprocal(out=rn[:], in_=prm_ps[:, 32:33])

        for j, vec in enumerate((bk, gk, bek, mk, vk)):
            nc.sync.dma_start(out=prow_bf[2 * j:2 * j + 2, :], in_=vec.rearrange("(c p) -> c p", p=P))
        nc.sync.dma_start(out=prow_bf[10:14, :], in_=bv.rearrange("(c p) -> c p", p=P))
        wsb = {}
        for m in W_ORDER:
            wsb[m] = keep.tile([P, 1024], BF16, name="wsb%d" % m)
            src = wv[m * P:(m + 1) * P, :] if m < 4 else wk[(m - 4) * P:(m - 3) * P, :]
            nc.sync.dma_start(out=wsb[m][:], in_=src)

        def channel_constants():
            nc.tensor.matmul(prm_ps[:, 0:31], lhsT=prow_bf[:], rhs=cmat[:, 0:31], start=True, stop=True)
            return prm_ps

        def channel_constants_scalar(prm_ps):
            nc.scalar.copy(out=prm[:, 0:31], in_=prm_ps[:, 0:31])
            rstd = keep.tile([P, 2], F32, name="rstd")
            nc.scalar.activation(out=rstd[:], in_=prm[:, 8:10], func=ACT.Abs_reciprocal_sqrt, bias=epst[:, 0:1], scale=1.0)
            for i in range(2):
                nc.scalar.activation(out=bn_scale[:, i:i + 1], in_=prm[:, 2 + i:3 + i], func=ACT.Copy, scale=rstd[:, i:i + 1])
            for i in range(2):
                nc.scalar.activation(out=bn_bias[:, i:i + 1], in_=prm[:, 17 + i:18 + i], func=ACT.Identity, bias=prm[:, 4 + i:5 + i], scale=bn_scale[:, i:i + 1])

        xp = keep.tile([P, 2, NB * NPX, 2], BF16, name="xp")
        xw = [None, keep.tile([P, 4, NB * NPX], BF16, name="xw1")]
        xc = [keep.tile([P, NCOL], U32, name="xc%d" % g, align_bytes=64) for g in range(2)]
        xs = [keep.tile([P, NCOL], U8, name="xs%d" % g, align_bytes=64) for g in range(2)]

        def widen(g, t):
            src_ap = xb[(g, t)][:].rearrange("p b n -> p (b n)").bitcast(FP8)
            col = sc[:, 4 * g + t:4 * g + t + 1]
            if g == 0:
                nc.vector.tensor_scalar(out=xp[:, t // 2, :, t % 2], in0=src_ap, scalar1=col, scalar2=None, op0=ALU.mult)
            else:
                nc.scalar.activation(out=xw[g][:, t, :], in_=src_ap, func=ACT.Copy, scale=col)

        def interleave_words():
            words = xp[:].rearrange("p u n e -> p (u n e)").bitcast(F32).rearrange("p (u q h w) -> p q h w u", u=2, q=4, h=12, w=24)
            for c0, r0, rstep, depth in CLASSES:
                for i in range(depth):
                    a = LAYER0[i] + c0
                    dst = xg[0][:, a:a + 192, :].rearrange("p c t -> p (c t)").bitcast(F32).rearrange("p (s q w u) -> p q s w u", q=4, s=2, w=24, u=2)
                    nc.vector.tensor_copy(out=dst, in_=words[:, :, r0 + i:r0 + i + rstep + 1:rstep, :, :])

        def interleave(g, scalar_share):
            rows = xw[g][:].rearrange("p t (q h w) -> p q h w t", q=4, h=12, w=24)
            for c, i in scalar_share:
                c0, r0, rstep, depth = CLASSES[c]
                a = LAYER0[i] + c0
                dst = xg[g][:, a:a + 192, :].rearrange("p (s q w) t -> p q s w t", q=4, s=2, w=24)
                for s in range(2):
                    nc.scalar.copy(out=dst[:, :, s], in_=rows[:, :, r0 + i + s * rstep, :, :])
            for c, (c0, r0, rstep, depth) in enumerate(CLASSES):
                for i in range(depth):
                    a = LAYER0[i] + c0
                    dst = xg[g][:, a:a + 192, :].rearrange("p (s q w) t -> p q s w t", q=4, s=2, w=24)
                    if (c, i) not in scalar_share:
                        nc.vector.tensor_copy(out=dst, in_=rows[:, :, r0 + i:r0 + i + rstep + 1:rstep, :, :])

        def quantize_x(g, a, b):
            nc.vector.quantize_mx(
                out=xc[g][:, a:b].bitcast(FP8X4),
                scales=xs[g][:, a:b],
                in_=xg[g][:, a:b, :].rearrange("p c t -> p (c t)"),
            )

        wg = keep.tile([P, 6, 2, P, 4], BF16, name="wg", align_bytes=64)
        wc = keep.tile([P, 6 * 2 * P], U32, name="wc", align_bytes=64)
        wsc = keep.tile([P, 6 * 2 * P], U8, name="wsc", align_bytes=64)
        wts = {}

        def transpose_w(m):
            words = wsb[m][:].bitcast(F32)
            wts[m] = bank("wt%d" % m)
            for g in range(2):
                for u in range(2):
                    j = 2 * g + u
                    nc.tensor.transpose(wts[m][:, j * P:(j + 1) * P], words[:, 256 * g + u:256 * (g + 1):2], ident[:])

        def copy_w(m):
            nc.scalar.copy(
                out=wg[:, m].rearrange("p g r t -> p (g r t)").bitcast(F32).rearrange("p (g r u) -> p g r u", g=2, u=2),
                in_=wts[m][:].rearrange("p (g u r) -> p g r u", g=2, u=2),
            )

        def quantize_w(m0, m1):
            nc.vector.quantize_mx(
                out=wc[:, m0 * 256:m1 * 256].bitcast(FP8X4),
                scales=wsc[:, m0 * 256:m1 * 256],
                in_=wg[:, m0:m1].rearrange("p m g r t -> p (m g r t)"),
            )

        def passes(out, m, g, offsets, n, start, stop):
            w0 = (2 * m + g) * P
            for idx, off in enumerate(offsets):
                nc.tensor.matmul_mx(
                    out=out,
                    lhsT=wc[:, w0:w0 + P].bitcast(FP8X4),
                    lhsT_scale=wsc[:, w0:w0 + P],
                    rhs=xc[g][:, off:off + n].bitcast(FP8X4),
                    rhs_scale=xs[g][:, off:off + n],
                    start=(start and idx == 0),
                    stop=(stop and idx == len(offsets) - 1),
                )

        def group(out, m, offsets, n):
            passes(out, m, 0, offsets, n, True, False)
            passes(out, m, 1, offsets, n, False, True)

        ev = keep.tile([P, 3, 4, 192], F32, name="ev")
        s8 = keep.tile([P, 6, NB, 64], F32, name="s8")
        s6 = keep.tile([P, 6, NB, 36], F32, name="s6")
        ek = [keep.tile([P, 3, 1, 192], F32, name="ek%d" % i) for i in range(2)]
        rk1 = [keep.tile([P, 2, 1, 192], F32, name="rk1_%d" % i) for i in range(2)]
        rk2 = [keep.tile([P, 1, 192], F32, name="rk2_%d" % i) for i in range(2)]
        kbank = {}

        def pool_big(src, m, o8):
            o6 = s6[:, m:m + 1].rearrange("p m b (h r w) -> p r (m b h) w", h=2, r=3, w=6)

            def red(out, in_, axis):
                return lambda: nc.vector.tensor_reduce(out=out, in_=in_, axis=axis, op=ALU.add)

            return [
                red(o8[:, 0:4:3], src[:, 0].rearrange("p m (e j) -> p (m e) j", j=3), AX.X),
                red(o6[:, 1], src[:, 1].rearrange("p m (s q w j) -> p (m q) w s j", q=4, s=2, w=6, j=4), AX.XY),
                red(o8[:, 1:3], src[:, 1:3].rearrange("p c m (e j) -> p (m e) c j", j=3), AX.XY),
                red(o6[:, 0:3:2], src[:, 0:3:2].rearrange("p c m (e j) -> p (m e) c j", j=4), AX.XY),
            ]

        def key_big(i):
            m = 4 + i
            return pool_big(ek[i][:], m, s8[:, m:m + 1].rearrange("p m b (h r w) -> p r (m b h) w", h=2, r=4, w=8))

        def value_big(m):
            return pool_big(ev[:, :, m:m + 1, :], m, ov[:, m:m + 1, :, 46:110].rearrange("p m b (h r w) -> p r (m b) h w", h=2, r=4, w=8))

        def sum3(m0, m1, out):
            nc.vector.tensor_reduce(
                out=out,
                in_=s6[:, m0:m1].rearrange("p m b (x a y c) -> p (m b x) y a c", x=3, a=2, y=3, c=2),
                axis=AX.XY, op=ALU.add,
            )

        def sum1(m0, m1, out):
            nc.vector.tensor_reduce(out=out, in_=s6[:, m0:m1].rearrange("p m b n -> p (m b) n"), axis=AX.X, op=ALU.add)

        def key_small(i):
            m = 4 + i
            return [
                lambda: sum3(m, m + 1, k3[:, i:i + 1].rearrange("p m b n -> p (m b) n")),
            ]

        def key_means(i):
            m = 4 + i
            nc.scalar.activation(out=okd[:, i, :, 46:110], in_=s8[:, m], func=ACT.Copy, scale=1.0 / 9.0)
            for b in range(NB):
                nc.scalar.activation(out=okd[:, i, b, 10:46], in_=s6[:, m, b, :], func=ACT.Copy, scale=1.0 / 16.0, accum_out=kacc[:, i, b, :])
            nc.scalar.activation(out=okd[:, i, :, 0:1], in_=kacc[:, i], func=ACT.Copy, scale=1.0 / 36.0)

        def key_store(i):
            nc.scalar.activation(out=okd[:, i, :, 1:10], in_=k3[:, i], func=ACT.Copy, scale=1.0 / 64.0)
            nc.scalar.dma_start(out=out_1.rearrange("b (i p) l -> i p b l", i=2)[i], in_=okd[:, i])

        def value_small(m0, m1):
            return [
                lambda: sum3(m0, m1, ov[:, m0:m1, :, 1:10].rearrange("p m b n -> p (m b) n")),
            ]

        def weave(main, extra):
            for idx in range(max(len(main), len(extra))):
                if idx < len(main):
                    main[idx]()
                if idx < len(extra):
                    extra[idx]()

        def value_tile(m):
            acc_a = bank("va%d" % m)
            acc_b = bank("vb%d" % m)
            group(acc_a[:, 0:256], m, (0, 640, 1024), 256)
            group(acc_a[:, 256:384], m, (256, 896), 128)
            group(acc_b[:, 0:256], m, (384,), 256)
            for c, src_ap in enumerate((acc_a[:, 0:192], acc_a[:, 192:384], acc_b[:, 0:192])):
                nc.scalar.activation(out=ev[:, c, m, :], in_=src_ap, func=ACT.Identity, bias=bd[:, c, m:m + 1], scale=1.0)

        KEY_WINDOWS = ((0, 512), (512, 512), (1024, 256))

        def key_passes(i, g):
            if g == 0:
                kbank[i] = [bank("k%d_%d" % (i, j)) for j in range(3)]
            for j in (0, 1, 2):
                off, n = KEY_WINDOWS[j]
                passes(kbank[i][j][:, 0:n], 4 + i, g, (off,), n, g == 0, g == 1)

        def key_relu(i):
            scale = bn_scale[:, i:i + 1]
            bias = bn_bias[:, i:i + 1]
            e_flat = ek[i][:].rearrange("p c i n -> p (c i n)")
            k1, k2, k3 = kbank[i]
            nc.scalar.activation(out=e_flat[:, 0:512], in_=k1[:, 0:512], func=ACT.Relu, bias=bias, scale=scale)
            nc.scalar.activation(out=rk1[i][:].rearrange("p c i n -> p (c i n)"), in_=k2[:, 128:512], func=ACT.Relu, bias=bias, scale=scale)
            nc.scalar.activation(out=e_flat[:, 512:576], in_=k2[:, 0:64], func=ACT.Relu, bias=bias, scale=scale)
            nc.scalar.activation(out=rk2[i][:].rearrange("p i n -> p (i n)"), in_=k3[:, 0:192], func=ACT.Relu, bias=bias, scale=scale)

        def key_adds(eng, i):
            flat = "p i n -> p (i n)"
            for c, other in ((0, rk1[i][:, 0]), (1, rk1[i][:, 1]), (0, rk2[i][:])):
                eng.tensor_tensor(out=ek[i][:, c].rearrange(flat), in0=ek[i][:, c].rearrange(flat), in1=other.rearrange(flat), op=ALU.add)

        pk = keep.tile([P, 288], F32, name="pk")
        g4 = keep.tile([P, 3, 48], F32, name="g4")
        a3 = keep.tile([P, 192], F32, name="a3")
        t12 = keep.tile([P, 2, 64], F32, name="t12")

        def gadd(out, in0, in1):
            nc.gpsimd.tensor_tensor(out=out, in0=in0, in1=in1, op=ALU.add)

        def key_pool_gpsimd(i):
            m = 4 + i
            e_all = ek[i][:].rearrange("p c i n -> p (c i n)")
            gadd(pk[:], e_all[:, 0:576:2], e_all[:, 1:576:2])
            gadd(g4[:].rearrange("p c n -> p (c n)"), pk[:, 0:288:2], pk[:, 1:288:2])
            o6 = s6[:, m:m + 1].rearrange("p m b (h r w) -> p (m b h) r w", h=2, r=3, w=6)
            shape6 = "p (s q w) -> p q s w"
            gadd(o6[:, :, 0:3:2, :], g4[:, 0].rearrange(shape6, q=4, s=2, w=6), g4[:, 2].rearrange(shape6, q=4, s=2, w=6))
            mid = g4[:, 1].rearrange(shape6, q=4, s=2, w=6)
            gadd(o6[:, :, 1, :], mid[:, :, 0, :], mid[:, :, 1, :])
            gadd(a3[:], e_all[:, 0:576:3], e_all[:, 1:576:3])
            o8 = s8[:, m:m + 1].rearrange("p m b (h r w) -> p (m b h) r w", h=2, r=4, w=8)
            shape8 = "p (s q w) -> p q s w"
            gadd(o8[:, :, 0:4:3, :], a3[:, 0:64].rearrange(shape8, q=4, s=2, w=8), e_all[:, 2:192:3].rearrange(shape8, q=4, s=2, w=8))
            gadd(t12[:].rearrange("p c n -> p (c n)"), a3[:, 64:192], e_all[:, 194:576:3])
            gadd(o8[:, :, 1:3, :], t12[:, 0].rearrange(shape8, q=4, s=2, w=8), t12[:, 1].rearrange(shape8, q=4, s=2, w=8))

        vt = [None, None]
        vlast = {}
        vo = keep.tile([P, NB, 512], F32, name="vo")

        def value_gather(m0, m1):
            for m in range(m0, m1):
                for b in range(NB):
                    nc.scalar.activation(out=ov[:, m, b, 10:46], in_=s6[:, m, b, :], func=ACT.Copy, accum_out=ov[:, m, b, 0:1])

        def value_turn():
            for b in range(NB):
                vt[b] = bank("vt%d" % b)
                for m in range(3):
                    nc.tensor.transpose(vt[b][:, m * P:(m + 1) * P], ov[:, m, b, :], ident[:])

        def value_evac(b, on_vector):
            if on_vector:
                nc.vector.tensor_scalar(out=vo[:, b, 0:3 * P], in0=vt[b][:, 0:3 * P], scalar1=rn[:, 0:1], scalar2=None, op0=ALU.mult)
            else:
                nc.scalar.activation(out=vo[:, b, 0:3 * P], in_=vt[b][:, 0:3 * P], func=ACT.Copy, scale=rn[:, 0:1])

        def value_store():
            nc.sync.dma_start(out=out_0.rearrange("b l c -> l b c")[:, :, 0:3 * P], in_=vo[0:NLOC, :, 0:3 * P])

        def value_turn_last():
            vlast["t"] = bank("vt3")
            for b in range(NB):
                nc.tensor.transpose(vlast["t"][:, b * P:(b + 1) * P], ov[:, 3, b, :], ident[:])

        def value_out_last():
            nc.vector.tensor_scalar(out=vo[:, :, 3 * P:4 * P], in0=vlast["t"][:, 0:2 * P].rearrange("p (b c) -> p b c", b=NB), scalar1=rn[:, 0:1], scalar2=None, op0=ALU.mult)
            nc.sync.dma_start(out=out_0.rearrange("b l c -> l b c")[:, :, 3 * P:4 * P], in_=vo[0:NLOC, :, 3 * P:4 * P])

        for t in range(4):
            widen(0, t)
        interleave_words()
        prm_bank = channel_constants()
        for t in range(4):
            widen(1, t)
        channel_constants_scalar(prm_bank)
        for m in W_ORDER:
            transpose_w(m)
        copy_w(4)
        copy_w(5)
        quantize_x(0, 1024, 1280)
        quantize_x(0, 0, 1024)
        interleave(1, S_SHARE)
        quantize_w(4, 6)
        key_passes(0, 0)
        for m in range(4):
            copy_w(m)
        quantize_x(1, 0, 512)
        quantize_x(1, 512, 1024)
        quantize_x(1, 1024, 1280)
        key_passes(0, 1)
        key_relu(0)
        quantize_w(0, 2)
        quantize_w(2, 4)
        key_passes(1, 0)
        key_passes(1, 1)
        key_relu(1)
        key_adds(nc.vector, 0)
        big = key_big(0)
        for idx in (1, 2, 0, 3):
            big[idx]()
        key_adds(nc.gpsimd, 1)
        key_pool_gpsimd(1)
        value_tile(0)
        value_tile(1)
        weave(value_big(0), key_small(0))
        value_tile(2)
        key_means(0)
        key_store(0)
        weave(value_big(1), [])
        value_tile(3)
        weave(value_big(2), [])
        big = value_big(3)
        weave(big[0:2], value_small(0, 3))
        value_gather(0, 3)
        value_turn()
        weave([big[3], big[2]], [])
        weave(value_small(3, 4), [])
        value_gather(3, 4)
        value_turn_last()
        weave(key_small(1), [])
        value_evac(0, True)
        value_evac(1, False)
        value_store()
        value_out_last()
        key_means(1)
        key_store(1)
